import numpy as np
import ml_dtypes


def mxq(x, axis, fmt="e4m3"):
    dtype, down = {"e4m3": (ml_dtypes.float8_e4m3fn, 7), "e5m2": (ml_dtypes.float8_e5m2, 14)}[fmt]
    v = np.moveaxis(np.asarray(x, np.float32).astype(ml_dtypes.bfloat16).astype(np.float64), axis, -1)
    blocks = v.reshape(v.shape[:-1] + (-1, 32))
    amax = np.abs(blocks).max(-1, keepdims=True)
    byte = np.maximum(np.where(amax > 0, np.frexp(amax)[1] - 1 + 127, 0) - down, 1)
    scale = np.exp2(byte - 127.0)
    codes = (blocks / scale).astype(np.float32).astype(dtype).astype(np.float64)
    return np.moveaxis((codes * scale).reshape(v.shape), -1, axis)


WIDE = False


def mx_kscale(k):
    if not WIDE:
        return np.ones(k)
    levels = np.array([10, -10, 5, -5, 0])
    a = np.random.permutation(np.resize(levels, k // 512 * 4)).reshape(k // 512, 4)
    idx = np.arange(k)
    return np.exp2(a[idx // 512, idx % 128 // 32])


BF16 = ml_dtypes.bfloat16


def bf(x):
    return np.asarray(x, np.float32).astype(BF16)


def f64(x):
    return np.asarray(x).astype(np.float64)


T, H, QR, NH, DN, DR, KVR = 512, 2048, 1536, 16, 128, 64, 448
EPS = 1e-6


def rmsnorm(x, gamma):
    var = np.mean(np.square(x), axis=-1, keepdims=True)
    return x * (1.0 / np.sqrt(var + EPS)) * gamma


def apply_rope(x, cos, sin):
    x1, x2 = np.split(x, 2, axis=-1)
    rot = np.concatenate([-x2, x1], axis=-1)
    return x * cos + rot * sin


def setup_inputs():
    s, t = mx_kscale(H), mx_kscale(QR)
    return {"token_x": bf(np.random.standard_normal((T, H)) * s),
            "wq_a": bf(np.random.standard_normal((H, QR)) / np.sqrt(H) / s[:, None]),
            "wq_b": bf(np.random.standard_normal((QR, NH * (DN + DR))) / np.sqrt(QR) / t[:, None]),
            "wkv": bf(np.random.standard_normal((H, KVR + DR)) / np.sqrt(H) / s[:, None]),
            "rope_cos": bf(np.random.uniform(-1.0, 1.0, (T, DR))),
            "rope_sin": bf(np.random.uniform(-1.0, 1.0, (T, DR))),
            "gamma_cq": bf((1.0 + 0.1 * np.random.standard_normal(QR)) * t),
            "gamma_ckv": bf(1.0 + 0.1 * np.random.standard_normal(KVR))}


def reference(token_x, wq_a, wq_b, wkv, rope_cos, rope_sin, gamma_cq, gamma_ckv):
    cos, sin = f64(rope_cos), f64(rope_sin)
    xq = mxq(f64(token_x), 1, "e4m3")
    cq = rmsnorm(xq @ mxq(f64(wq_a), 0, "e4m3"), f64(gamma_cq))
    q = (mxq(cq, 1, "e4m3") @ mxq(f64(wq_b), 0, "e4m3")).reshape(T, NH, DN + DR)
    q_nope, q_rope = q[..., :DN], q[..., DN:]
    q_rope = apply_rope(q_rope, cos[:, None, :], sin[:, None, :])
    query = np.concatenate([q_nope, q_rope], axis=-1)
    kv = xq @ mxq(f64(wkv), 0, "e4m3")
    ckv = rmsnorm(kv[:, :KVR], f64(gamma_ckv))
    k_rope = apply_rope(kv[:, KVR:], cos, sin)
    return np.concatenate([query.reshape(T, -1), ckv, k_rope], axis=-1)

@@ -1,0 +1,294 @@
+from contextlib import ExitStack
+
+import concourse.mybir as mybir
+from concourse.masks import make_identity
+
+F32 = mybir.dt.float32
+BF16 = mybir.dt.bfloat16
+U32 = mybir.dt.uint32
+U8 = mybir.dt.uint8
+FP8X4 = mybir.dt.float8_e4m3fn_x4
+ALU = mybir.AluOpType
+ACT = mybir.ActivationFunctionType
+AX = mybir.AxisListType
+
+P = 128
+T, H, QR, NQ, KV, KVR, DR = 512, 2048, 1536, 3072, 512, 448, 64
+EPS = 1e-6
+FLOPS = 2 * T * (H * QR + QR * NQ + H * KV)
+
+STREAM = ((0, 0), (0, 1), (0, 2), (1, 0), (1, 1), (1, 2), (2, 0), (2, 1))
+LATE = ((2, 2), (3, 0), (3, 1), (3, 2))
+ROPE_SLOT = (2, 0, 1)
+
+
+def tile_mla_model_kernel(
+    tc, token_x, wq_a, wq_b, wkv, rope_cos, rope_sin, gamma_cq, gamma_ckv, out
+):
+    nc = tc.nc
+    with ExitStack() as ctx:
+        const = ctx.enter_context(tc.tile_pool(name="const", bufs=1))
+        keep = ctx.enter_context(tc.tile_pool(name="keep", bufs=1))
+        raw_pool = ctx.enter_context(tc.tile_pool(name="raw", bufs=4))
+        r4_pool = ctx.enter_context(tc.tile_pool(name="r4", bufs=4))
+        grp_pool = ctx.enter_context(tc.tile_pool(name="grp", bufs=4))
+        work = ctx.enter_context(tc.tile_pool(name="work", bufs=3))
+        cq_pool = ctx.enter_context(tc.tile_pool(name="cqp", bufs=2))
+        stat = ctx.enter_context(tc.tile_pool(name="stat", bufs=4))
+        outp = ctx.enter_context(tc.tile_pool(name="outp", bufs=6))
+        psum = ctx.enter_context(tc.psum_pool(name="psum", bufs=8))
+
+        eps = const.tile([P, 1], F32, name="eps")
+        nc.vector.memset(eps[:], EPS)
+        warm = const.tile([P, 1], F32, name="warm")
+        nc.scalar.activation(out=warm[:], in_=eps[:], func=ACT.Sqrt)
+        ident_f = const.tile([P, P], F32, name="ident_f")
+        make_identity(nc, ident_f[:])
+        ident_b = const.tile([P, P], BF16, name="ident_b")
+        make_identity(nc, ident_b[:])
+
+        cosb = const.tile([P, 4, DR], BF16, name="cosb")
+        nc.scalar.dma_start(out=cosb[:], in_=rope_cos.rearrange("(t p) d -> p t d", p=P))
+        sinb = const.tile([P, 4, DR], BF16, name="sinb")
+        nc.scalar.dma_start(out=sinb[:], in_=rope_sin.rearrange("(t p) d -> p t d", p=P))
+        gam_q = const.tile([P, QR], BF16, name="gam_q")
+        nc.scalar.dma_start(out=gam_q[:], in_=gamma_cq.partition_broadcast(P))
+        gam_k = const.tile([P, KVR], BF16, name="gam_k")
+        nc.scalar.dma_start(out=gam_k[:], in_=gamma_ckv.partition_broadcast(P))
+
+        tab_a = const.tile([P, 4, DR], F32, name="tab_a")
+        tab_b = const.tile([P, 4, DR], F32, name="tab_b")
+        nc.gpsimd.tensor_copy(out=tab_a[:, :, 0:32], in_=cosb[:, :, 0:32])
+        nc.gpsimd.tensor_copy(out=tab_a[:, :, 32:64], in_=sinb[:, :, 32:64])
+        nc.gpsimd.tensor_scalar(
+            out=tab_b[:, :, 0:32], in0=sinb[:, :, 0:32], scalar1=-1.0, scalar2=0.0,
+            op0=ALU.mult, op1=ALU.add,
+        )
+        nc.gpsimd.tensor_copy(out=tab_b[:, :, 32:64], in_=cosb[:, :, 32:64])
+
+        xc = keep.tile([P, 4, 512], U32, name="xc", align_bytes=64)
+        xs = keep.tile([P, 4, 512], U8, name="xs", align_bytes=64)
+        wa_c = [keep.tile([P, QR], U32, name="wa_c%d" % g, align_bytes=64) for g in range(4)]
+        wa_s = [keep.tile([P, QR], U8, name="wa_s%d" % g, align_bytes=64) for g in range(4)]
+        wk_c = keep.tile([P, 4, 512], U32, name="wk_c", align_bytes=64)
+        wk_s = keep.tile([P, 4, 512], U8, name="wk_s", align_bytes=64)
+        wb_c = [keep.tile([P, QR], U32, name="wb_c%d" % i, align_bytes=64) for i in range(6)]
+        wb_s = [keep.tile([P, QR], U8, name="wb_s%d" % i, align_bytes=64) for i in range(6)]
+        cqc = keep.tile([P, 4, 384], U32, name="cqc", align_bytes=64)
+        cqs = keep.tile([P, 4, 384], U8, name="cqs", align_bytes=64)
+
+        unit_count = [0]
+
+        def quantise_unit(src, codes, scales):
+            on_scalar = unit_count[0] % 2 == 1
+            unit_count[0] += 1
+            wg = grp_pool.tile([P, 2048], BF16, tag="grp", name="wg", align_bytes=64)
+            dst = wg[:].rearrange("p (c i t) -> p c t i", i=4, t=4)
+            view = src.rearrange("p t (c i) -> p c t i", i=4)
+            if on_scalar:
+                nc.scalar.copy(out=dst, in_=view)
+            else:
+                nc.vector.tensor_copy(out=dst, in_=view)
+            nc.vector.quantize_mx(out=codes.bitcast(FP8X4), scales=scales, in_=wg[:])
+
+        for t in range(4):
+            xr = r4_pool.tile([P, H], BF16, tag="r4", name="xr")
+            nc.sync.dma_start(out=xr[:], in_=token_x[t * P:(t + 1) * P, :])
+            x32 = xr[:].bitcast(F32)
+            xg = grp_pool.tile([P, 2048], BF16, tag="grp", name="xg", align_bytes=64)
+            xg32 = xg[:].bitcast(F32)
+            for gp in range(2):
+                xt = psum.tile([P, 4, P], F32, tag="bank", name="xt")
+                for i in range(4):
+                    w0 = 512 * gp + P * i
+                    nc.tensor.transpose(out=xt[:, i, :], in_=x32[:, w0:w0 + P], identity=ident_f[:])
+                dst = xg32[:, 512 * gp:512 * gp + 512].rearrange("p (g r u) -> p g r u", g=2, u=2)
+                view = xt[:].rearrange("p (g u) r -> p g r u", u=2)
+                if gp == 0:
+                    nc.vector.tensor_copy(out=dst, in_=view)
+                else:
+                    nc.scalar.copy(out=dst, in_=view)
+            nc.vector.quantize_mx(out=xc[:, t, :].bitcast(FP8X4), scales=xs[:, t, :], in_=xg[:])
+
+        a_bank = {}
+
+        def stage1_pass(t, c, g):
+            cols = slice(512 * c, 512 * c + 512)
+            nc.tensor.matmul_mx(
+                out=a_bank[(t, c)][:],
+                lhsT=xc[:, t, P * g:P * g + P].bitcast(FP8X4),
+                lhsT_scale=xs[:, t, P * g:P * g + P],
+                rhs=wa_c[g][:, cols].bitcast(FP8X4),
+                rhs_scale=wa_s[g][:, cols],
+                start=(g == 0),
+                stop=(g == 3),
+            )
+
+        for g in range(4):
+            rw = raw_pool.tile([P, 4, QR], BF16, tag="raw", name="rw")
+            nc.sync.dma_start(
+                out=rw[:].rearrange("p (u e) c -> p u e c", u=2),
+                in_=wq_a[512 * g:512 * g + 512, :].rearrange("(u q e) c -> q u e c", u=2, e=2),
+            )
+            for c in range(3):
+                cols = slice(512 * c, 512 * c + 512)
+                quantise_unit(rw[:, :, cols], wa_c[g][:, cols], wa_s[g][:, cols])
+                for t in range(4):
+                    if (t, c) in STREAM:
+                        if g == 0:
+                            a_bank[(t, c)] = psum.tile([P, 512], F32, tag="bank", name="a_bank")
+                        stage1_pass(t, c, g)
+
+        cq_tiles = {}
+
+        def norm_scale(t):
+            ssq = stat.tile([P, 4], F32, tag="ssq", name="ssq")
+            for c in range(3):
+                junk = work.tile([P, 512], BF16, tag="junk", name="junk")
+                nc.scalar.activation(
+                    out=junk[:], in_=a_bank[(t, c)][:], func=ACT.Square, accum_out=ssq[:, c:c + 1]
+                )
+            ss = stat.tile([P, 1], F32, tag="ss", name="ss")
+            nc.vector.tensor_reduce(out=ss[:], in_=ssq[:, 0:3], axis=AX.X, op=ALU.add)
+            rms = stat.tile([P, 1], F32, tag="rms", name="rms")
+            nc.scalar.activation(out=rms[:], in_=ss[:], func=ACT.Sqrt, bias=eps[:, 0:1], scale=1.0 / QR)
+            rstd = stat.tile([P, 1], F32, tag="rstd", name="rstd")
+            nc.vector.reciprocal(out=rstd[:], in_=rms[:])
+            cq = cq_pool.tile([P, QR], BF16, tag="cq", name="cq")
+            for c in range(3):
+                cols = slice(512 * c, 512 * c + 512)
+                nc.vector.scalar_tensor_tensor(
+                    out=cq[:, cols], in0=a_bank[(t, c)][:], scalar=rstd[:, 0:1], in1=gam_q[:, cols],
+                    op0=ALU.mult, op1=ALU.mult,
+                )
+            cq_tiles[t] = cq
+
+        def transpose_cq(t):
+            cq = cq_tiles[t]
+            for g in range(3):
+                tp = psum.tile([P, 4, P], BF16, tag="bank", name="tp")
+                for j in range(4):
+                    k0 = 512 * g + P * j
+                    nc.tensor.transpose(out=tp[:, j, :], in_=cq[:, k0:k0 + P], identity=ident_b[:])
+                cg = work.tile([P, 512], BF16, tag="cg", name="cg", align_bytes=64)
+                nc.scalar.copy(
+                    out=cg[:].rearrange("p (r j) -> p r j", j=4), in_=tp[:].rearrange("p j r -> p r j")
+                )
+                nc.vector.quantize_mx(
+                    out=cqc[:, t, P * g:P * g + P].bitcast(FP8X4),
+                    scales=cqs[:, t, P * g:P * g + P],
+                    in_=cg[:],
+                )
+
+        def late_bank(t, c):
+            a_bank[(t, c)] = psum.tile([P, 512], F32, tag="bank", name="a_bank")
+            for g in range(4):
+                stage1_pass(t, c, g)
+
+        def rope(bank, ot, s0, t):
+            nb = len(range(s0, 8, 3))
+            b32 = bank[:].rearrange("p (s w) -> p s w", w=32)
+            shape = [P, nb, 2, 32]
+            x1 = b32[:, 2 * s0:16:6, :].unsqueeze(2).to_broadcast(shape)
+            x2 = b32[:, 2 * s0 + 1:16:6, :].unsqueeze(2).to_broadcast(shape)
+            ta = tab_a[:, t, :].rearrange("p (h w) -> p h w", h=2).unsqueeze(1).to_broadcast(shape)
+            tb = tab_b[:, t, :].rearrange("p (h w) -> p h w", h=2).unsqueeze(1).to_broadcast(shape)
+            pa = work.tile([P, 3, 2, 32], F32, tag="pa", name="pa")
+            pb = work.tile([P, 3, 2, 32], F32, tag="pb", name="pb")
+            nc.vector.tensor_tensor(out=pa[:, 0:nb], in0=x1, in1=ta, op=ALU.mult)
+            nc.vector.tensor_tensor(out=pb[:, 0:nb], in0=x2, in1=tb, op=ALU.mult)
+            o64 = ot[:].rearrange("p (s h w) -> p s h w", h=2, w=32)
+            nc.vector.tensor_tensor(out=o64[:, s0:8:3], in0=pa[:, 0:nb], in1=pb[:, 0:nb], op=ALU.add)
+
+        norm_scale(0)
+        late_bank(2, 2)
+        norm_scale(1)
+        late_bank(3, 0)
+        late_bank(3, 1)
+        late_bank(3, 2)
+        transpose_cq(0)
+        transpose_cq(1)
+        norm_scale(2)
+        transpose_cq(2)
+        norm_scale(3)
+        transpose_cq(3)
+
+        for g in range(4):
+            rk = r4_pool.tile([P, 4, 512], BF16, tag="r4", name="rk")
+            nc.sync.dma_start(
+                out=rk[:].rearrange("p (u e) c -> p u e c", u=2),
+                in_=wkv[512 * g:512 * g + 512, :].rearrange("(u q e) c -> q u e c", u=2, e=2),
+            )
+            quantise_unit(rk[:], wk_c[:, g, :], wk_s[:, g, :])
+        for t in range(4):
+            kvb = psum.tile([P, 512], F32, tag="bank", name="kvb")
+            for g in range(4):
+                nc.tensor.matmul_mx(
+                    out=kvb[:],
+                    lhsT=xc[:, t, P * g:P * g + P].bitcast(FP8X4),
+                    lhsT_scale=xs[:, t, P * g:P * g + P],
+                    rhs=wk_c[:, g, :].bitcast(FP8X4),
+                    rhs_scale=wk_s[:, g, :],
+                    start=(g == 0),
+                    stop=(g == 3),
+                )
+            ssk = stat.tile([P, 1], F32, tag="ss", name="ssk")
+            junk = work.tile([P, 512], BF16, tag="junk", name="junk")
+            nc.scalar.activation(
+                out=junk[:, 0:KVR], in_=kvb[:, 0:KVR], func=ACT.Square, accum_out=ssk[:]
+            )
+            rmk = stat.tile([P, 1], F32, tag="rms", name="rmk")
+            nc.scalar.activation(out=rmk[:], in_=ssk[:], func=ACT.Sqrt, bias=eps[:, 0:1], scale=1.0 / KVR)
+            rsk = stat.tile([P, 1], F32, tag="rstd", name="rsk")
+            nc.vector.reciprocal(out=rsk[:], in_=rmk[:])
+            ot = outp.tile([P, 512], F32, tag="ot", name="ot")
+            nc.vector.scalar_tensor_tensor(
+                out=ot[:, 0:KVR], in0=kvb[:, 0:KVR], scalar=rsk[:, 0:1], in1=gam_k[:],
+                op0=ALU.mult, op1=ALU.mult,
+            )
+            rope(kvb, ot, 7, t)
+            nc.sync.dma_start(out=out[t * P:(t + 1) * P, NQ:NQ + KV], in_=ot[:])
+
+        def load_b(hf, g):
+            rb = raw_pool.tile([P, 4, QR], BF16, tag="raw", name="rb")
+            nc.sync.dma_start(
+                out=rb[:],
+                in_=wq_b[512 * g:512 * g + 512, QR * hf:QR * hf + QR].rearrange("(j p) n -> p j n", p=P),
+            )
+            return rb
+
+        def unit_b(rb, hf, g, c):
+            cols = slice(512 * c, 512 * c + 512)
+            quantise_unit(rb[:, :, cols], wb_c[3 * hf + g][:, cols], wb_s[3 * hf + g][:, cols])
+
+        for hf in range(2):
+            for g in range(2):
+                rb = load_b(hf, g)
+                for c in range(3):
+                    unit_b(rb, hf, g, c)
+            rb = load_b(hf, 2)
+            for c in range(3):
+                unit_b(rb, hf, 2, c)
+                cols = slice(512 * c, 512 * c + 512)
+                s0 = ROPE_SLOT[c]
+                for t in range(4):
+                    qb = psum.tile([P, 512], F32, tag="bank", name="qb")
+                    for g in range(3):
+                        nc.tensor.matmul_mx(
+                            out=qb[:],
+                            lhsT=cqc[:, t, P * g:P * g + P].bitcast(FP8X4),
+                            lhsT_scale=cqs[:, t, P * g:P * g + P],
+                            rhs=wb_c[3 * hf + g][:, cols].bitcast(FP8X4),
+                            rhs_scale=wb_s[3 * hf + g][:, cols],
+                            start=(g == 0),
+                            stop=(g == 2),
+                        )
+                    ot = outp.tile([P, 512], F32, tag="ot", name="ot")
+                    q64 = qb[:].rearrange("p (s w) -> p s w", w=64)
+                    o64 = ot[:].rearrange("p (s w) -> p s w", w=64)
+                    for r in range(3):
+                        if r != s0 % 3:
+                            nc.scalar.copy(out=o64[:, r:8:3, :], in_=q64[:, r:8:3, :])
+                    rope(qb, ot, s0, t)
+                    col0 = QR * hf + 512 * c
+                    nc.sync.dma_start(out=out[t * P:(t + 1) * P, col0:col0 + 512], in_=ot[:])

@@ -18,8 +18,35 @@ EPS = 1e-6
 FLOPS = 2 * T * (H * QR + QR * NQ + H * KV)
 
 STREAM = ((0, 0), (0, 1), (0, 2), (1, 0), (1, 1), (1, 2), (2, 0), (2, 1))
-LATE = ((2, 2), (3, 0), (3, 1), (3, 2))
 ROPE_SLOT = (2, 0, 1)
+ENG_A = "VSVSVSVSVSVS"
+ENG_K = "VVVV"
+ENG_B = "SVSSVSSVSSVSSVSSVS"
+ENG_TC = "SSSSVV"
+PINNED = True
+SEQ = (
+    "XP0", "XC00", "GB2", "GB1", "XP1", "XC10", "XP2", "XC01", "XC11", "XC21", "RV", "ZZ",
+    "XC20", "XZ0", "RV", "MM", "GB3", "XZ2", "XZ1", "XP3", "XC31", "RS", "ZZ", "GB0",
+    "RV", "ZZ", "ZZ", "KM2", "XC30", "MM", "RS", "KM1", "XZ3", "RV", "KS2", "RV",
+    "KM3", "ZZ", "ZZ", "KS1", "ZZ", "KS3", "MM", "KF1", "MM", "KM0", "RV", "KS0",
+    "MM", "RS", "MM", "RS", "KF3", "KF2", "ZZ", "KD2", "MM", "ZZ", "RS", "RV",
+    "MM", "KF0", "ZZ", "ZZ", "ZZ", "RV", "RS", "ZZ", "ZZ", "RV", "ZZ", "MM",
+    "MM", "MM", "MM", "RS", "MM", "MM", "SQ00", "MM", "KD0", "SQ20", "ZZ", "MM",
+    "SQ01", "SQ02", "ST0", "SQ12", "SQ10", "LB22", "LB32", "LB31", "KD1", "SQ11", "SQ21", "SQ22",
+    "RV", "ST1", "LB30", "KD3", "ZZ", "SQ32", "SC0", "ST2", "RV", "ZZ", "RS", "SC1",
+    "TT1", "SQ30", "SC2", "TT0", "TT3", "SQ31", "ST3", "TT2", "RV", "ZZ", "SC3", "TT4",
+    "CS3", "CV4", "CS1", "TZ1", "TZ3", "TT5", "CS0", "RS", "TZ0", "CV2", "TZ2", "CS5",
+    "TZ4", "ZZ", "MM", "TZ5", "RV", "MM", "MM", "RS", "ZZ", "RV", "MM", "EN01",
+    "EA01", "MM", "ZZ", "RS", "RV", "RS", "MM", "EA00", "EN00", "ZZ", "EA10", "ED01",
+    "EN02", "EN03", "ZZ", "EN11", "RS", "ED00", "EN13", "EN10", "ZZ", "ZZ", "ED10", "MM",
+    "EA11", "RS", "EA03", "ED03", "ZZ", "EA02", "MM", "ZZ", "ED02", "ED11", "RV", "MM",
+    "EA13", "EA23", "MM", "EN22", "EN21", "EA22", "EN23", "ZZ", "EN12", "MM", "ED13", "ZZ",
+    "EA21", "RS", "MM", "ED21", "ED23", "EA12", "EN31", "ED12", "EA32", "EA31", "ED22", "RS",
+    "ZZ", "ED31", "EN32", "ED32", "EA30", "EA20", "EA33", "MM", "EN30", "MM", "ED30", "RV",
+    "EN33", "ZZ", "MM", "MM", "ZZ", "ED33", "EN43", "EA43", "EA40", "RS", "EN41", "ED43",
+    "ZZ", "EN42", "EA41", "EN40", "MM", "ED40", "ED41", "EN20", "ED20", "MM", "EA42", "ED42",
+    "EA51", "EN51", "EN52", "EA50", "ED51", "EN50", "ED50", "EN53", "EA52", "ED52", "EA53", "ED53",
+)
 
 
 def tile_mla_model_kernel(
@@ -27,19 +54,33 @@ def tile_mla_model_kernel(
 ):
     nc = tc.nc
     with ExitStack() as ctx:
+        if PINNED:
+            ctx.enter_context(tc.manual_schedule())
         const = ctx.enter_context(tc.tile_pool(name="const", bufs=1))
         keep = ctx.enter_context(tc.tile_pool(name="keep", bufs=1))
-        raw_pool = ctx.enter_context(tc.tile_pool(name="raw", bufs=4))
-        r4_pool = ctx.enter_context(tc.tile_pool(name="r4", bufs=4))
-        grp_pool = ctx.enter_context(tc.tile_pool(name="grp", bufs=4))
+        raw_pool = ctx.enter_context(tc.tile_pool(name="raw", bufs=6))
+        wcp = ctx.enter_context(tc.tile_pool(name="wcp", bufs=6))
+        r4_pool = ctx.enter_context(tc.tile_pool(name="r4", bufs=5))
+        grp_pool = ctx.enter_context(tc.tile_pool(name="grp", bufs=6))
         work = ctx.enter_context(tc.tile_pool(name="work", bufs=3))
-        cq_pool = ctx.enter_context(tc.tile_pool(name="cqp", bufs=2))
+        junkp = ctx.enter_context(tc.tile_pool(name="junkp", bufs=2))
+        cgp = ctx.enter_context(tc.tile_pool(name="cgp", bufs=4))
+        cq_pool = ctx.enter_context(tc.tile_pool(name="cqp", bufs=3))
         stat = ctx.enter_context(tc.tile_pool(name="stat", bufs=4))
-        outp = ctx.enter_context(tc.tile_pool(name="outp", bufs=6))
+        outp = ctx.enter_context(tc.tile_pool(name="outp", bufs=7))
         psum = ctx.enter_context(tc.psum_pool(name="psum", bufs=8))
+
+        x_view = token_x.rearrange("(p t) h -> p t h", t=4)
+        out_view = out.rearrange("(p t) n -> p t n", t=4)
 
         eps = const.tile([P, 1], F32, name="eps")
         nc.vector.memset(eps[:], EPS)
+        zrow = grp_pool.tile([P, 2048], BF16, tag="grp", name="zrow", align_bytes=64)
+        nc.vector.memset(zrow[:], 0.0)
+        ones = const.tile([P, P], BF16, name="ones")
+        nc.vector.memset(ones[:], 1.0)
+        cosb = const.tile([P, 4, DR], BF16, name="cosb")
+        sinb = const.tile([P, 4, DR], BF16, name="sinb")
         warm = const.tile([P, 1], F32, name="warm")
         nc.scalar.activation(out=warm[:], in_=eps[:], func=ACT.Sqrt)
         ident_f = const.tile([P, P], F32, name="ident_f")
@@ -47,14 +88,35 @@ def tile_mla_model_kernel(
         ident_b = const.tile([P, P], BF16, name="ident_b")
         make_identity(nc, ident_b[:])
 
-        cosb = const.tile([P, 4, DR], BF16, name="cosb")
-        nc.scalar.dma_start(out=cosb[:], in_=rope_cos.rearrange("(t p) d -> p t d", p=P))
-        sinb = const.tile([P, 4, DR], BF16, name="sinb")
-        nc.scalar.dma_start(out=sinb[:], in_=rope_sin.rearrange("(t p) d -> p t d", p=P))
-        gam_q = const.tile([P, QR], BF16, name="gam_q")
-        nc.scalar.dma_start(out=gam_q[:], in_=gamma_cq.partition_broadcast(P))
-        gam_k = const.tile([P, KVR], BF16, name="gam_k")
-        nc.scalar.dma_start(out=gam_k[:], in_=gamma_ckv.partition_broadcast(P))
+        xr = []
+        rks = []
+
+        def load_x(t, pieces):
+            xr.append(r4_pool.tile([P, H], BF16, tag="r4", name="xr%d" % t))
+            wid = H // pieces
+            for i in range(pieces):
+                nc.sync.dma_start(out=xr[t][:, wid * i:wid * i + wid], in_=x_view[:, t, wid * i:wid * i + wid])
+
+        def load_k(g):
+            rk = r4_pool.tile([P, 4, 512], BF16, tag="r4", name="rk%d" % g)
+            nc.sync.dma_start(
+                out=rk[:].rearrange("p (u e) c -> p u e c", u=2),
+                in_=wkv[512 * g:512 * g + 512, :].rearrange("(u q e) c -> q u e c", u=2, e=2),
+            )
+            rks.append(rk)
+
+        load_x(0, 2)
+        load_x(1, 1)
+        nc.sync.dma_start(out=zrow[0:1, 0:QR], in_=gamma_cq.unsqueeze(0))
+        nc.sync.dma_start(out=zrow[0:1, QR:QR + KVR], in_=gamma_ckv.unsqueeze(0))
+        nc.sync.dma_start(out=cosb[:], in_=rope_cos.rearrange("(p t) d -> p t d", t=4))
+        nc.sync.dma_start(out=sinb[:], in_=rope_sin.rearrange("(p t) d -> p t d", t=4))
+        load_k(0)
+        load_x(2, 1)
+        load_k(1)
+        load_x(3, 1)
+        load_k(2)
+        load_k(3)
 
         tab_a = const.tile([P, 4, DR], F32, name="tab_a")
         tab_b = const.tile([P, 4, DR], F32, name="tab_b")
@@ -68,49 +130,61 @@ def tile_mla_model_kernel(
 
         xc = keep.tile([P, 4, 512], U32, name="xc", align_bytes=64)
         xs = keep.tile([P, 4, 512], U8, name="xs", align_bytes=64)
-        wa_c = [keep.tile([P, QR], U32, name="wa_c%d" % g, align_bytes=64) for g in range(4)]
-        wa_s = [keep.tile([P, QR], U8, name="wa_s%d" % g, align_bytes=64) for g in range(4)]
         wk_c = keep.tile([P, 4, 512], U32, name="wk_c", align_bytes=64)
         wk_s = keep.tile([P, 4, 512], U8, name="wk_s", align_bytes=64)
-        wb_c = [keep.tile([P, QR], U32, name="wb_c%d" % i, align_bytes=64) for i in range(6)]
-        wb_s = [keep.tile([P, QR], U8, name="wb_s%d" % i, align_bytes=64) for i in range(6)]
         cqc = keep.tile([P, 4, 384], U32, name="cqc", align_bytes=64)
         cqs = keep.tile([P, 4, 384], U8, name="cqs", align_bytes=64)
+        gam_q = const.tile([P, QR], BF16, name="gam_q")
+        gam_k = const.tile([P, 512], BF16, name="gam_k")
 
-        unit_count = [0]
-
-        def quantise_unit(src, codes, scales):
-            on_scalar = unit_count[0] % 2 == 1
-            unit_count[0] += 1
-            wg = grp_pool.tile([P, 2048], BF16, tag="grp", name="wg", align_bytes=64)
-            dst = wg[:].rearrange("p (c i t) -> p c t i", i=4, t=4)
-            view = src.rearrange("p t (c i) -> p c t i", i=4)
-            if on_scalar:
-                nc.scalar.copy(out=dst, in_=view)
+        units = []
+        for g in range(4):
+            units.append((rks[g][:], wk_c[:, g, :], wk_s[:, g, :], "V", ("K", g, 0)))
+        wa_c, wa_s = [], []
+        for g in range(4):
+            rw = raw_pool.tile([P, 4, QR], BF16, tag="raw", name="rw%d" % g)
+            if g == 0:
+                for c in range(3):
+                    for u in range(2):
+                        r0 = 256 * u
+                        nc.sync.dma_start(
+                            out=rw[:, 2 * u:2 * u + 2, 512 * c:512 * c + 512],
+                            in_=wq_a[r0:r0 + 256, 512 * c:512 * c + 512].rearrange("(q e) c -> q e c", e=2),
+                        )
             else:
-                nc.vector.tensor_copy(out=dst, in_=view)
-            nc.vector.quantize_mx(out=codes.bitcast(FP8X4), scales=scales, in_=wg[:])
-
-        for t in range(4):
-            xr = r4_pool.tile([P, H], BF16, tag="r4", name="xr")
-            nc.sync.dma_start(out=xr[:], in_=token_x[t * P:(t + 1) * P, :])
-            x32 = xr[:].bitcast(F32)
-            xg = grp_pool.tile([P, 2048], BF16, tag="grp", name="xg", align_bytes=64)
-            xg32 = xg[:].bitcast(F32)
-            for gp in range(2):
-                xt = psum.tile([P, 4, P], F32, tag="bank", name="xt")
-                for i in range(4):
-                    w0 = 512 * gp + P * i
-                    nc.tensor.transpose(out=xt[:, i, :], in_=x32[:, w0:w0 + P], identity=ident_f[:])
-                dst = xg32[:, 512 * gp:512 * gp + 512].rearrange("p (g r u) -> p g r u", g=2, u=2)
-                view = xt[:].rearrange("p (g u) r -> p g r u", u=2)
-                if gp == 0:
-                    nc.vector.tensor_copy(out=dst, in_=view)
-                else:
-                    nc.scalar.copy(out=dst, in_=view)
-            nc.vector.quantize_mx(out=xc[:, t, :].bitcast(FP8X4), scales=xs[:, t, :], in_=xg[:])
+                nc.sync.dma_start(
+                    out=rw[:].rearrange("p (u e) c -> p u e c", u=2),
+                    in_=wq_a[512 * g:512 * g + 512, :].rearrange("(u q e) c -> q u e c", u=2, e=2),
+                )
+            wa_c.append(wcp.tile([P, QR], U32, tag="wc", name="wa_c%d" % g, align_bytes=64))
+            wa_s.append(wcp.tile([P, QR], U8, tag="ws", name="wa_s%d" % g, align_bytes=64))
+            for c in range(3):
+                cols = slice(512 * c, 512 * c + 512)
+                units.append((rw[:, :, cols], wa_c[g][:, cols], wa_s[g][:, cols], ENG_A[3 * g + c], ("A", g, c)))
+        wb_c, wb_s = {}, {}
+        for hf in range(2):
+            rbs = []
+            for g in range(3):
+                rb = raw_pool.tile([P, 4, QR], BF16, tag="raw", name="rb%d%d" % (hf, g))
+                nc.sync.dma_start(
+                    out=rb[:],
+                    in_=wq_b[512 * g:512 * g + 512, QR * hf:QR * hf + QR].rearrange("(j p) n -> p j n", p=P),
+                )
+                rbs.append(rb)
+                wb_c[(hf, g)] = wcp.tile([P, QR], U32, tag="wc", name="wb_c%d%d" % (hf, g), align_bytes=64)
+                wb_s[(hf, g)] = wcp.tile([P, QR], U8, tag="ws", name="wb_s%d%d" % (hf, g), align_bytes=64)
+            for c in range(3):
+                cols = slice(512 * c, 512 * c + 512)
+                for g in range(3):
+                    units.append((
+                        rbs[g][:, :, cols], wb_c[(hf, g)][:, cols], wb_s[(hf, g)][:, cols],
+                        ENG_B[9 * hf + 3 * c + g], ("B", 3 * hf + c, g),
+                    ))
 
         a_bank = {}
+        q_bank = {}
+        grouped = {}
+        pos = {"r": 0, "z": 0, "m": 0}
 
         def stage1_pass(t, c, g):
             cols = slice(512 * c, 512 * c + 512)
@@ -124,68 +198,168 @@ def tile_mla_model_kernel(
                 stop=(g == 3),
             )
 
-        for g in range(4):
-            rw = raw_pool.tile([P, 4, QR], BF16, tag="raw", name="rw")
-            nc.sync.dma_start(
-                out=rw[:].rearrange("p (u e) c -> p u e c", u=2),
-                in_=wq_a[512 * g:512 * g + 512, :].rearrange("(u q e) c -> q u e c", u=2, e=2),
-            )
-            for c in range(3):
-                cols = slice(512 * c, 512 * c + 512)
-                quantise_unit(rw[:, :, cols], wa_c[g][:, cols], wa_s[g][:, cols])
+        def passes_after(what):
+            kind, i, j = what
+            if kind == "A":
+                g, c = i, j
                 for t in range(4):
                     if (t, c) in STREAM:
                         if g == 0:
-                            a_bank[(t, c)] = psum.tile([P, 512], F32, tag="bank", name="a_bank")
+                            a_bank[(t, c)] = psum.tile([P, 512], F32, tag="bank", name="a%d%d" % (t, c))
                         stage1_pass(t, c, g)
+            if kind == "B":
+                s, g = i, j
+                hf, c = divmod(s, 3)
+                cols = slice(512 * c, 512 * c + 512)
+                for t in range(4):
+                    if g == 0:
+                        q_bank[(s, t)] = psum.tile([P, 512], F32, tag="bank", name="q%d%d" % (s, t))
+                    nc.tensor.matmul_mx(
+                        out=q_bank[(s, t)][:],
+                        lhsT=cqc[:, t, P * g:P * g + P].bitcast(FP8X4),
+                        lhsT_scale=cqs[:, t, P * g:P * g + P],
+                        rhs=wb_c[(hf, g)][:, cols].bitcast(FP8X4),
+                        rhs_scale=wb_s[(hf, g)][:, cols],
+                        start=(g == 0),
+                        stop=(g == 2),
+                    )
+
+        def regroup_next(eng):
+            k = pos["r"]
+            if k >= len(units):
+                return
+            pos["r"] = k + 1
+            src, codes, scales, unused, what = units[k]
+            wg = grp_pool.tile([P, 2048], BF16, tag="grp", name="wg%d" % k, align_bytes=64)
+            grouped[k] = wg
+            dst = wg[:].rearrange("p (c i t) -> p c t i", i=4, t=4)
+            view = src.rearrange("p t (c i) -> p c t i", i=4)
+            if eng == "S":
+                nc.scalar.copy(out=dst, in_=view)
+            else:
+                nc.vector.tensor_copy(out=dst, in_=view)
+
+        def quantise_next():
+            k = pos["z"]
+            if k >= len(units):
+                return
+            pos["z"] = k + 1
+            src, codes, scales, eng, what = units[k]
+            nc.vector.quantize_mx(out=codes.bitcast(FP8X4), scales=scales, in_=grouped[k][:])
+
+        def passes_next():
+            k = pos["m"]
+            assert k < pos["z"]
+            pos["m"] = k + 1
+            passes_after(units[k][4])
+
+        xg = {}
+
+        xts = {}
+
+        def x_transpose(t):
+            x32 = xr[t][:].bitcast(F32)
+            xg[t] = grp_pool.tile([P, 2048], BF16, tag="grp", name="xg%d" % t, align_bytes=64)
+            for gp in range(2):
+                xt = psum.tile([P, 4, P], F32, tag="bank", name="xt%d%d" % (t, gp))
+                xts[(t, gp)] = xt
+                for i in range(4):
+                    w0 = 512 * gp + P * i
+                    nc.tensor.transpose(out=xt[:, i, :], in_=x32[:, w0:w0 + P], identity=ident_f[:])
+
+        def x_copy(t, gp, eng):
+            xg32 = xg[t][:].bitcast(F32)
+            dst = xg32[:, 512 * gp:512 * gp + 512].rearrange("p (g r u) -> p g r u", g=2, u=2)
+            view = xts[(t, gp)][:].rearrange("p (g u) r -> p g r u", u=2)
+            if eng == "S":
+                nc.scalar.copy(out=dst, in_=view)
+            else:
+                nc.vector.tensor_copy(out=dst, in_=view)
+
+        def x_quantise(t):
+            nc.vector.quantize_mx(out=xc[:, t, :].bitcast(FP8X4), scales=xs[:, t, :], in_=xg[t][:])
+
+        def spread_gains(c):
+            gb = psum.tile([P, 512], F32, tag="bank", name="gb%d" % c)
+            nc.tensor.matmul(out=gb[:], lhsT=ones[:], rhs=zrow[:, 512 * c:512 * c + 512], start=True, stop=True)
+            if c < 3:
+                nc.scalar.copy(out=gam_q[:, 512 * c:512 * c + 512], in_=gb[:])
+            else:
+                nc.scalar.copy(out=gam_k[:], in_=gb[:])
+
 
         cq_tiles = {}
+        ssq = {}
+        rstd = {}
+        rms = {}
 
-        def norm_scale(t):
-            ssq = stat.tile([P, 4], F32, tag="ssq", name="ssq")
-            for c in range(3):
-                junk = work.tile([P, 512], BF16, tag="junk", name="junk")
+        def squares(t, cs):
+            if t not in ssq:
+                ssq[t] = stat.tile([P, 4], F32, tag="ssq", name="ssq%d" % t)
+            for c in cs:
+                junk = junkp.tile([P, 512], BF16, tag="junk", name="junk")
                 nc.scalar.activation(
-                    out=junk[:], in_=a_bank[(t, c)][:], func=ACT.Square, accum_out=ssq[:, c:c + 1]
+                    out=junk[:], in_=a_bank[(t, c)][:], func=ACT.Square, accum_out=ssq[t][:, c:c + 1]
                 )
-            ss = stat.tile([P, 1], F32, tag="ss", name="ss")
-            nc.vector.tensor_reduce(out=ss[:], in_=ssq[:, 0:3], axis=AX.X, op=ALU.add)
-            rms = stat.tile([P, 1], F32, tag="rms", name="rms")
-            nc.scalar.activation(out=rms[:], in_=ss[:], func=ACT.Sqrt, bias=eps[:, 0:1], scale=1.0 / QR)
-            rstd = stat.tile([P, 1], F32, tag="rstd", name="rstd")
-            nc.vector.reciprocal(out=rstd[:], in_=rms[:])
-            cq = cq_pool.tile([P, QR], BF16, tag="cq", name="cq")
+
+        def stats(t):
+            ss = stat.tile([P, 1], F32, tag="ss", name="ss%d" % t)
+            j3 = stat.tile([P, 4], F32, tag="j3", name="j3")
+            nc.scalar.activation(out=j3[:, 0:3], in_=ssq[t][:, 0:3], func=ACT.Copy, accum_out=ss[:])
+            rms[t] = stat.tile([P, 1], F32, tag="rms", name="rms%d" % t)
+            nc.scalar.activation(out=rms[t][:], in_=ss[:], func=ACT.Sqrt, bias=eps[:, 0:1], scale=1.0 / QR)
+
+        def scale_cq(t):
+            rstd[t] = stat.tile([P, 1], F32, tag="rstd", name="rstd%d" % t)
+            nc.vector.reciprocal(out=rstd[t][:], in_=rms[t][:])
+            cq = cq_pool.tile([P, QR], BF16, tag="cq", name="cq%d" % t)
             for c in range(3):
                 cols = slice(512 * c, 512 * c + 512)
                 nc.vector.scalar_tensor_tensor(
-                    out=cq[:, cols], in0=a_bank[(t, c)][:], scalar=rstd[:, 0:1], in1=gam_q[:, cols],
+                    out=cq[:, cols], in0=a_bank[(t, c)][:], scalar=rstd[t][:, 0:1], in1=gam_q[:, cols],
                     op0=ALU.mult, op1=ALU.mult,
                 )
             cq_tiles[t] = cq
 
-        def transpose_cq(t):
-            cq = cq_tiles[t]
-            for g in range(3):
-                tp = psum.tile([P, 4, P], BF16, tag="bank", name="tp")
+        cgs = {}
+        tps = {}
+        cqc_flat = cqc[:].rearrange("p t w -> p (t w)")
+        cqs_flat = cqs[:].rearrange("p t w -> p (t w)")
+
+        def cq_transpose(pair):
+            tp = psum.tile([P, 8, P], BF16, tag="bank", name="tp%d" % pair)
+            tps[pair] = tp
+            for h in range(2):
+                t, g = divmod(2 * pair + h, 3)
                 for j in range(4):
                     k0 = 512 * g + P * j
-                    nc.tensor.transpose(out=tp[:, j, :], in_=cq[:, k0:k0 + P], identity=ident_b[:])
-                cg = work.tile([P, 512], BF16, tag="cg", name="cg", align_bytes=64)
-                nc.scalar.copy(
-                    out=cg[:].rearrange("p (r j) -> p r j", j=4), in_=tp[:].rearrange("p j r -> p r j")
-                )
-                nc.vector.quantize_mx(
-                    out=cqc[:, t, P * g:P * g + P].bitcast(FP8X4),
-                    scales=cqs[:, t, P * g:P * g + P],
-                    in_=cg[:],
-                )
+                    nc.tensor.transpose(out=tp[:, 4 * h + j, :], in_=cq_tiles[t][:, k0:k0 + P], identity=ident_b[:])
+
+        def cq_copy(pair, eng):
+            cg = cgp.tile([P, 1024], BF16, tag="cg", name="cg%d" % pair, align_bytes=64)
+            cgs[pair] = cg
+            dst = cg[:].rearrange("p (h r j) -> p h r j", h=2, j=4)
+            view = tps[pair][:].rearrange("p (h j) r -> p h r j", h=2)
+            if eng == "S":
+                nc.scalar.copy(out=dst, in_=view)
+            else:
+                nc.vector.tensor_copy(out=dst, in_=view)
+
+        def cq_quantise(pair):
+            nc.vector.quantize_mx(
+                out=cqc_flat[:, 256 * pair:256 * pair + 256].bitcast(FP8X4),
+                scales=cqs_flat[:, 256 * pair:256 * pair + 256],
+                in_=cgs[pair][:],
+            )
 
         def late_bank(t, c):
-            a_bank[(t, c)] = psum.tile([P, 512], F32, tag="bank", name="a_bank")
+            a_bank[(t, c)] = psum.tile([P, 512], F32, tag="bank", name="a%d%d" % (t, c))
             for g in range(4):
                 stage1_pass(t, c, g)
 
-        def rope(bank, ot, s0, t):
+        prod = {}
+
+        def rope_products(key, bank, s0, t):
             nb = len(range(s0, 8, 3))
             b32 = bank[:].rearrange("p (s w) -> p s w", w=32)
             shape = [P, nb, 2, 32]
@@ -197,34 +371,23 @@ def tile_mla_model_kernel(
             pb = work.tile([P, 3, 2, 32], F32, tag="pb", name="pb")
             nc.vector.tensor_tensor(out=pa[:, 0:nb], in0=x1, in1=ta, op=ALU.mult)
             nc.vector.tensor_tensor(out=pb[:, 0:nb], in0=x2, in1=tb, op=ALU.mult)
+            prod[key] = (pa, pb, nb, s0)
+
+        def rope_sum(key, ot):
+            pa, pb, nb, s0 = prod[key]
             o64 = ot[:].rearrange("p (s h w) -> p s h w", h=2, w=32)
             nc.vector.tensor_tensor(out=o64[:, s0:8:3], in0=pa[:, 0:nb], in1=pb[:, 0:nb], op=ALU.add)
 
-        norm_scale(0)
-        late_bank(2, 2)
-        norm_scale(1)
-        late_bank(3, 0)
-        late_bank(3, 1)
-        late_bank(3, 2)
-        transpose_cq(0)
-        transpose_cq(1)
-        norm_scale(2)
-        transpose_cq(2)
-        norm_scale(3)
-        transpose_cq(3)
+        kv_bank = {}
+        ots = {}
+        rsk = {}
+        rmk = {}
 
-        for g in range(4):
-            rk = r4_pool.tile([P, 4, 512], BF16, tag="r4", name="rk")
-            nc.sync.dma_start(
-                out=rk[:].rearrange("p (u e) c -> p u e c", u=2),
-                in_=wkv[512 * g:512 * g + 512, :].rearrange("(u q e) c -> q u e c", u=2, e=2),
-            )
-            quantise_unit(rk[:], wk_c[:, g, :], wk_s[:, g, :])
-        for t in range(4):
-            kvb = psum.tile([P, 512], F32, tag="bank", name="kvb")
+        def kv_passes(t):
+            kv_bank[t] = psum.tile([P, 512], F32, tag="bank", name="kv%d" % t)
             for g in range(4):
                 nc.tensor.matmul_mx(
-                    out=kvb[:],
+                    out=kv_bank[t][:],
                     lhsT=xc[:, t, P * g:P * g + P].bitcast(FP8X4),
                     lhsT_scale=xs[:, t, P * g:P * g + P],
                     rhs=wk_c[:, g, :].bitcast(FP8X4),
@@ -232,63 +395,97 @@ def tile_mla_model_kernel(
                     start=(g == 0),
                     stop=(g == 3),
                 )
-            ssk = stat.tile([P, 1], F32, tag="ss", name="ssk")
-            junk = work.tile([P, 512], BF16, tag="junk", name="junk")
+
+        def kv_stats(t):
+            ssk = stat.tile([P, 1], F32, tag="ss", name="ssk%d" % t)
+            junk = junkp.tile([P, 512], BF16, tag="junk", name="junk")
             nc.scalar.activation(
-                out=junk[:, 0:KVR], in_=kvb[:, 0:KVR], func=ACT.Square, accum_out=ssk[:]
+                out=junk[:, 0:KVR], in_=kv_bank[t][:, 0:KVR], func=ACT.Square, accum_out=ssk[:]
             )
-            rmk = stat.tile([P, 1], F32, tag="rms", name="rmk")
-            nc.scalar.activation(out=rmk[:], in_=ssk[:], func=ACT.Sqrt, bias=eps[:, 0:1], scale=1.0 / KVR)
-            rsk = stat.tile([P, 1], F32, tag="rstd", name="rsk")
-            nc.vector.reciprocal(out=rsk[:], in_=rmk[:])
-            ot = outp.tile([P, 512], F32, tag="ot", name="ot")
+            rmk[t] = stat.tile([P, 1], F32, tag="rms", name="rmk%d" % t)
+            nc.scalar.activation(out=rmk[t][:], in_=ssk[:], func=ACT.Sqrt, bias=eps[:, 0:1], scale=1.0 / KVR)
+
+        def kv_finish(t):
+            rsk[t] = stat.tile([P, 1], F32, tag="rstd", name="rsk%d" % t)
+            nc.vector.reciprocal(out=rsk[t][:], in_=rmk[t][:])
+            ot = outp.tile([P, 512], F32, tag="ot", name="otk%d" % t)
             nc.vector.scalar_tensor_tensor(
-                out=ot[:, 0:KVR], in0=kvb[:, 0:KVR], scalar=rsk[:, 0:1], in1=gam_k[:],
+                out=ot[:, 0:KVR], in0=kv_bank[t][:, 0:KVR], scalar=rsk[t][:, 0:1], in1=gam_k[:, 0:KVR],
                 op0=ALU.mult, op1=ALU.mult,
             )
-            rope(kvb, ot, 7, t)
-            nc.sync.dma_start(out=out[t * P:(t + 1) * P, NQ:NQ + KV], in_=ot[:])
+            rope_products(("k", t), kv_bank[t], 7, t)
+            ots[("k", t)] = ot
 
-        def load_b(hf, g):
-            rb = raw_pool.tile([P, 4, QR], BF16, tag="raw", name="rb")
-            nc.sync.dma_start(
-                out=rb[:],
-                in_=wq_b[512 * g:512 * g + 512, QR * hf:QR * hf + QR].rearrange("(j p) n -> p j n", p=P),
-            )
-            return rb
+        def kv_store(t):
+            rope_sum(("k", t), ots[("k", t)])
+            nc.sync.dma_start(out=out_view[:, t, NQ:NQ + KV], in_=ots[("k", t)][:])
 
-        def unit_b(rb, hf, g, c):
-            cols = slice(512 * c, 512 * c + 512)
-            quantise_unit(rb[:, :, cols], wb_c[3 * hf + g][:, cols], wb_s[3 * hf + g][:, cols])
+        def nope_out(s, t):
+            s0 = ROPE_SLOT[s % 3]
+            ot = outp.tile([P, 512], F32, tag="ot", name="ot%d%d" % (s, t))
+            ots[(s, t)] = ot
+            q64 = q_bank[(s, t)][:].rearrange("p (s w) -> p s w", w=64)
+            o64 = ot[:].rearrange("p (s w) -> p s w", w=64)
+            for r in range(3):
+                if r != s0 % 3:
+                    nc.scalar.copy(out=o64[:, r:8:3, :], in_=q64[:, r:8:3, :])
 
-        for hf in range(2):
-            for g in range(2):
-                rb = load_b(hf, g)
-                for c in range(3):
-                    unit_b(rb, hf, g, c)
-            rb = load_b(hf, 2)
-            for c in range(3):
-                unit_b(rb, hf, 2, c)
-                cols = slice(512 * c, 512 * c + 512)
-                s0 = ROPE_SLOT[c]
-                for t in range(4):
-                    qb = psum.tile([P, 512], F32, tag="bank", name="qb")
-                    for g in range(3):
-                        nc.tensor.matmul_mx(
-                            out=qb[:],
-                            lhsT=cqc[:, t, P * g:P * g + P].bitcast(FP8X4),
-                            lhsT_scale=cqs[:, t, P * g:P * g + P],
-                            rhs=wb_c[3 * hf + g][:, cols].bitcast(FP8X4),
-                            rhs_scale=wb_s[3 * hf + g][:, cols],
-                            start=(g == 0),
-                            stop=(g == 2),
-                        )
-                    ot = outp.tile([P, 512], F32, tag="ot", name="ot")
-                    q64 = qb[:].rearrange("p (s w) -> p s w", w=64)
-                    o64 = ot[:].rearrange("p (s w) -> p s w", w=64)
-                    for r in range(3):
-                        if r != s0 % 3:
-                            nc.scalar.copy(out=o64[:, r:8:3, :], in_=q64[:, r:8:3, :])
-                    rope(qb, ot, s0, t)
-                    col0 = QR * hf + 512 * c
-                    nc.sync.dma_start(out=out[t * P:(t + 1) * P, col0:col0 + 512], in_=ot[:])
+        def store(s, t):
+            rope_sum((s, t), ots[(s, t)])
+            nc.sync.dma_start(out=out_view[:, t, 512 * s:512 * s + 512], in_=ots[(s, t)][:])
+
+        def run(tok):
+            op, a = tok[:2], [int(ch) for ch in tok[2:] if ch in "0123456789"]
+            if op == "RV":
+                regroup_next("V")
+            elif op == "RS":
+                regroup_next("S")
+            elif op == "ZZ":
+                quantise_next()
+            elif op == "XP":
+                x_transpose(a[0])
+            elif op == "XC":
+                x_copy(a[0], a[1], "S")
+            elif op == "XD":
+                x_copy(a[0], a[1], "V")
+            elif op == "XZ":
+                x_quantise(a[0])
+            elif op == "GB":
+                spread_gains(a[0])
+            elif op == "MM":
+                passes_next()
+            elif op == "SQ":
+                squares(a[0], (a[1],))
+            elif op == "ST":
+                stats(a[0])
+            elif op == "SC":
+                scale_cq(a[0])
+            elif op == "LB":
+                late_bank(a[0], a[1])
+            elif op == "TT":
+                cq_transpose(a[0])
+            elif op == "CV":
+                cq_copy(a[0], "V")
+            elif op == "CS":
+                cq_copy(a[0], "S")
+            elif op == "TZ":
+                cq_quantise(a[0])
+            elif op == "KM":
+                kv_passes(a[0])
+            elif op == "KS":
+                kv_stats(a[0])
+            elif op == "KF":
+                kv_finish(a[0])
+            elif op == "KD":
+                kv_store(a[0])
+            elif op == "EN":
+                nope_out(a[0], a[1])
+            elif op == "EA":
+                rope_products((a[0], a[1]), q_bank[(a[0], a[1])], ROPE_SLOT[a[0] % 3], a[1])
+            elif op == "ED":
+                store(a[0], a[1])
+            else:
+                raise ValueError(tok)
+
+        for tok in SEQ:
+            run(tok)

@@ -25,27 +25,27 @@ ENG_B = "SVSSVSSVSSVSSVSSVS"
 ENG_TC = "SSSSVV"
 PINNED = True
 SEQ = (
-    "XP0", "XC00", "GB2", "GB1", "XP1", "XC10", "XP2", "XC01", "XC11", "XC21", "RV", "ZZ",
-    "XC20", "XZ0", "RV", "MM", "GB3", "XZ2", "XZ1", "XP3", "XC31", "RS", "ZZ", "GB0",
-    "RV", "ZZ", "ZZ", "KM2", "XC30", "MM", "RS", "KM1", "XZ3", "RV", "KS2", "RV",
-    "KM3", "ZZ", "ZZ", "KS1", "ZZ", "KS3", "MM", "KF1", "MM", "KM0", "RV", "KS0",
-    "MM", "RS", "MM", "RS", "KF3", "KF2", "ZZ", "KD2", "MM", "ZZ", "RS", "RV",
-    "MM", "KF0", "ZZ", "ZZ", "ZZ", "RV", "RS", "ZZ", "ZZ", "RV", "ZZ", "MM",
-    "MM", "MM", "MM", "RS", "MM", "MM", "SQ00", "MM", "KD0", "SQ20", "ZZ", "MM",
-    "SQ01", "SQ02", "ST0", "SQ12", "SQ10", "LB22", "LB32", "LB31", "KD1", "SQ11", "SQ21", "SQ22",
-    "RV", "ST1", "LB30", "KD3", "ZZ", "SQ32", "SC0", "ST2", "RV", "ZZ", "RS", "SC1",
-    "TT1", "SQ30", "SC2", "TT0", "TT3", "SQ31", "ST3", "TT2", "RV", "ZZ", "SC3", "TT4",
-    "CS3", "CV4", "CS1", "TZ1", "TZ3", "TT5", "CS0", "RS", "TZ0", "CV2", "TZ2", "CS5",
-    "TZ4", "ZZ", "MM", "TZ5", "RV", "MM", "MM", "RS", "ZZ", "RV", "MM", "EN01",
-    "EA01", "MM", "ZZ", "RS", "RV", "RS", "MM", "EA00", "EN00", "ZZ", "EA10", "ED01",
-    "EN02", "EN03", "ZZ", "EN11", "RS", "ED00", "EN13", "EN10", "ZZ", "ZZ", "ED10", "MM",
-    "EA11", "RS", "EA03", "ED03", "ZZ", "EA02", "MM", "ZZ", "ED02", "ED11", "RV", "MM",
-    "EA13", "EA23", "MM", "EN22", "EN21", "EA22", "EN23", "ZZ", "EN12", "MM", "ED13", "ZZ",
-    "EA21", "RS", "MM", "ED21", "ED23", "EA12", "EN31", "ED12", "EA32", "EA31", "ED22", "RS",
-    "ZZ", "ED31", "EN32", "ED32", "EA30", "EA20", "EA33", "MM", "EN30", "MM", "ED30", "RV",
-    "EN33", "ZZ", "MM", "MM", "ZZ", "ED33", "EN43", "EA43", "EA40", "RS", "EN41", "ED43",
-    "ZZ", "EN42", "EA41", "EN40", "MM", "ED40", "ED41", "EN20", "ED20", "MM", "EA42", "ED42",
-    "EA51", "EN51", "EN52", "EA50", "ED51", "EN50", "ED50", "EN53", "EA52", "ED52", "EA53", "ED53",
+    "RV", "XP0", "RV", "XP1", "XC00", "XC11", "ZZ", "XP2", "XC01", "RS", "ZZ", "XP3",
+    "XD10", "XC20", "XZ0", "XC21", "XD30", "RV", "ZZ", "ZZ", "XZ1", "XC31", "XZ2", "XZ3",
+    "MM", "MM", "RS", "KM0", "GB0", "KM2", "KS2", "KS0", "RV", "RV", "ZZ", "KM1",
+    "RV", "GB3", "RV", "GB1", "KS1", "GB2", "MM", "KM3", "RV", "KF2", "KF1", "ZZ",
+    "MM", "KF0", "RS", "KS3", "MM", "ZZ", "MM", "RS", "MM", "ZZ", "KD0", "MM",
+    "KF3", "ZZ", "MM", "ZZ", "MM", "ZZ", "RS", "ZZ", "MM", "MM", "RV", "ZZ",
+    "MM", "RS", "ZZ", "RV", "MM", "ZZ", "SQ10", "SQ00", "ZZ", "MM", "MM", "RV",
+    "LB22", "LB31", "RV", "SQ01", "SQ02", "ST0", "SC0", "SQ11", "SQ12", "ST1", "KD1", "SQ21",
+    "SQ20", "SQ22", "ZZ", "ST2", "RS", "LB30", "SC1", "TT1", "SQ30", "LB32", "SC2", "ZZ",
+    "TT3", "TT0", "KD2", "CV1", "TT2", "SQ31", "TZ1", "SQ32", "ST3", "SC3", "CS0", "TT4",
+    "CS3", "ZZ", "CV4", "TZ0", "TZ3", "KD3", "TT5", "CS2", "RS", "TZ4", "MM", "TZ2",
+    "RV", "CS5", "RS", "ZZ", "TZ5", "ZZ", "MM", "MM", "RV", "RV", "MM", "MM",
+    "RS", "EA00", "EN03", "EN02", "ZZ", "EA01", "EN00", "MM", "ED00", "RV", "RS", "EA03",
+    "EN11", "EA02", "ED03", "ZZ", "MM", "ZZ", "ZZ", "RS", "EN10", "ED02", "EA11", "ED11",
+    "ZZ", "MM", "RS", "ZZ", "EN01", "ZZ", "EA12", "MM", "MM", "EN12", "EA10", "ED12",
+    "ED10", "EA20", "EN20", "EA13", "MM", "EN23", "MM", "RS", "ZZ", "EN13", "ED01", "EN22",
+    "ED20", "EA21", "EA23", "RV", "EN32", "EN21", "ED21", "RS", "EN33", "RS", "MM", "ZZ",
+    "EA22", "ED22", "ED13", "ZZ", "ED23", "EA31", "EA30", "EA32", "EN30", "EN31", "MM", "MM",
+    "ZZ", "ED32", "EN42", "MM", "ED30", "EA33", "ED33", "RV", "ZZ", "EN43", "EN41", "ZZ",
+    "EN40", "ED31", "MM", "EA42", "MM", "EA43", "ED42", "EN51", "EA40", "ED40", "EA41", "ED41",
+    "EN50", "EN53", "EA51", "ED51", "ED43", "EA53", "ED53", "EA50", "ED50", "EN52", "EA52", "ED52",
 )
 
 
@@ -105,28 +105,10 @@ def tile_mla_model_kernel(
             )
             rks.append(rk)
 
-        load_x(0, 2)
-        load_x(1, 1)
-        nc.sync.dma_start(out=zrow[0:1, 0:QR], in_=gamma_cq.unsqueeze(0))
-        nc.sync.dma_start(out=zrow[0:1, QR:QR + KVR], in_=gamma_ckv.unsqueeze(0))
-        nc.sync.dma_start(out=cosb[:], in_=rope_cos.rearrange("(p t) d -> p t d", t=4))
-        nc.sync.dma_start(out=sinb[:], in_=rope_sin.rearrange("(p t) d -> p t d", t=4))
-        load_k(0)
-        load_x(2, 1)
-        load_k(1)
-        load_x(3, 1)
-        load_k(2)
-        load_k(3)
+        for t in range(4):
+            load_x(t, 1)
+            load_k(t)
 
-        tab_a = const.tile([P, 4, DR], F32, name="tab_a")
-        tab_b = const.tile([P, 4, DR], F32, name="tab_b")
-        nc.gpsimd.tensor_copy(out=tab_a[:, :, 0:32], in_=cosb[:, :, 0:32])
-        nc.gpsimd.tensor_copy(out=tab_a[:, :, 32:64], in_=sinb[:, :, 32:64])
-        nc.gpsimd.tensor_scalar(
-            out=tab_b[:, :, 0:32], in0=sinb[:, :, 0:32], scalar1=-1.0, scalar2=0.0,
-            op0=ALU.mult, op1=ALU.add,
-        )
-        nc.gpsimd.tensor_copy(out=tab_b[:, :, 32:64], in_=cosb[:, :, 32:64])
 
         xc = keep.tile([P, 4, 512], U32, name="xc", align_bytes=64)
         xs = keep.tile([P, 4, 512], U8, name="xs", align_bytes=64)
@@ -143,19 +125,15 @@ def tile_mla_model_kernel(
         wa_c, wa_s = [], []
         for g in range(4):
             rw = raw_pool.tile([P, 4, QR], BF16, tag="raw", name="rw%d" % g)
+            nc.sync.dma_start(
+                out=rw[:].rearrange("p (u e) c -> p u e c", u=2),
+                in_=wq_a[512 * g:512 * g + 512, :].rearrange("(u q e) c -> q u e c", u=2, e=2),
+            )
             if g == 0:
-                for c in range(3):
-                    for u in range(2):
-                        r0 = 256 * u
-                        nc.sync.dma_start(
-                            out=rw[:, 2 * u:2 * u + 2, 512 * c:512 * c + 512],
-                            in_=wq_a[r0:r0 + 256, 512 * c:512 * c + 512].rearrange("(q e) c -> q e c", e=2),
-                        )
-            else:
-                nc.sync.dma_start(
-                    out=rw[:].rearrange("p (u e) c -> p u e c", u=2),
-                    in_=wq_a[512 * g:512 * g + 512, :].rearrange("(u q e) c -> q u e c", u=2, e=2),
-                )
+                nc.sync.dma_start(out=zrow[0:1, 0:QR], in_=gamma_cq.unsqueeze(0))
+                nc.sync.dma_start(out=zrow[0:1, QR:QR + KVR], in_=gamma_ckv.unsqueeze(0))
+                nc.sync.dma_start(out=cosb[:], in_=rope_cos.rearrange("(p t) d -> p t d", t=4))
+                nc.sync.dma_start(out=sinb[:], in_=rope_sin.rearrange("(p t) d -> p t d", t=4))
             wa_c.append(wcp.tile([P, QR], U32, tag="wc", name="wa_c%d" % g, align_bytes=64))
             wa_s.append(wcp.tile([P, QR], U8, tag="ws", name="wa_s%d" % g, align_bytes=64))
             for c in range(3):
@@ -180,6 +158,16 @@ def tile_mla_model_kernel(
                         rbs[g][:, :, cols], wb_c[(hf, g)][:, cols], wb_s[(hf, g)][:, cols],
                         ENG_B[9 * hf + 3 * c + g], ("B", 3 * hf + c, g),
                     ))
+
+        tab_a = const.tile([P, 4, DR], F32, name="tab_a")
+        tab_b = const.tile([P, 4, DR], F32, name="tab_b")
+        nc.gpsimd.tensor_copy(out=tab_a[:, :, 0:32], in_=cosb[:, :, 0:32])
+        nc.gpsimd.tensor_copy(out=tab_a[:, :, 32:64], in_=sinb[:, :, 32:64])
+        nc.gpsimd.tensor_scalar(
+            out=tab_b[:, :, 0:32], in0=sinb[:, :, 0:32], scalar1=-1.0, scalar2=0.0,
+            op0=ALU.mult, op1=ALU.add,
+        )
+        nc.gpsimd.tensor_copy(out=tab_b[:, :, 32:64], in_=cosb[:, :, 32:64])
 
         a_bank = {}
         q_bank = {}

@@ -10,43 +10,22 @@ U8 = mybir.dt.uint8
 FP8X4 = mybir.dt.float8_e4m3fn_x4
 ALU = mybir.AluOpType
 ACT = mybir.ActivationFunctionType
-AX = mybir.AxisListType
 
 P = 128
+TILES = 4
 T, H, QR, NQ, KV, KVR, DR = 512, 2048, 1536, 3072, 512, 448, 64
+HALF = DR // 2
+W = 512
 EPS = 1e-6
 FLOPS = 2 * T * (H * QR + QR * NQ + H * KV)
 
-STREAM = ((0, 0), (0, 1), (0, 2), (1, 0), (1, 1), (1, 2), (2, 0), (2, 1))
-ROPE_SLOT = (2, 0, 1)
-ENG_A = "VSVSVSVSVSVS"
-ENG_K = "VVVV"
-ENG_B = "SVSSVSSVSSVSSVSSVS"
-ENG_TC = "SSSSVV"
-PINNED = True
-SEQ = (
-    "RV", "XP0", "RV", "XP1", "XC00", "XC11", "ZZ", "XP2", "XC01", "RS", "ZZ", "XP3",
-    "XD10", "XC20", "XZ0", "XC21", "XD30", "RV", "ZZ", "ZZ", "XZ1", "XC31", "XZ2", "XZ3",
-    "MM", "MM", "RS", "KM0", "GB0", "KM2", "KS2", "KS0", "RV", "RV", "ZZ", "KM1",
-    "RV", "GB3", "RV", "GB1", "KS1", "GB2", "MM", "KM3", "RV", "KF2", "KF1", "ZZ",
-    "MM", "KF0", "RS", "KS3", "MM", "ZZ", "MM", "RS", "MM", "ZZ", "KD0", "MM",
-    "KF3", "ZZ", "MM", "ZZ", "MM", "ZZ", "RS", "ZZ", "MM", "MM", "RV", "ZZ",
-    "MM", "RS", "ZZ", "RV", "MM", "ZZ", "SQ10", "SQ00", "ZZ", "MM", "MM", "RV",
-    "LB22", "LB31", "RV", "SQ01", "SQ02", "ST0", "SC0", "SQ11", "SQ12", "ST1", "KD1", "SQ21",
-    "SQ20", "SQ22", "ZZ", "ST2", "RS", "LB30", "SC1", "TT1", "SQ30", "LB32", "SC2", "ZZ",
-    "TT3", "TT0", "KD2", "CV1", "TT2", "SQ31", "TZ1", "SQ32", "ST3", "SC3", "CS0", "TT4",
-    "CS3", "ZZ", "CV4", "TZ0", "TZ3", "KD3", "TT5", "CS2", "RS", "TZ4", "MM", "TZ2",
-    "RV", "CS5", "RS", "ZZ", "TZ5", "ZZ", "MM", "MM", "RV", "RV", "MM", "MM",
-    "RS", "EA00", "EN03", "EN02", "ZZ", "EA01", "EN00", "MM", "ED00", "RV", "RS", "EA03",
-    "EN11", "EA02", "ED03", "ZZ", "MM", "ZZ", "ZZ", "RS", "EN10", "ED02", "EA11", "ED11",
-    "ZZ", "MM", "RS", "ZZ", "EN01", "ZZ", "EA12", "MM", "MM", "EN12", "EA10", "ED12",
-    "ED10", "EA20", "EN20", "EA13", "MM", "EN23", "MM", "RS", "ZZ", "EN13", "ED01", "EN22",
-    "ED20", "EA21", "EA23", "RV", "EN32", "EN21", "ED21", "RS", "EN33", "RS", "MM", "ZZ",
-    "EA22", "ED22", "ED13", "ZZ", "ED23", "EA31", "EA30", "EA32", "EN30", "EN31", "MM", "MM",
-    "ZZ", "ED32", "EN42", "MM", "ED30", "EA33", "ED33", "RV", "ZZ", "EN43", "EN41", "ZZ",
-    "EN40", "ED31", "MM", "EA42", "MM", "EA43", "ED42", "EN51", "EA40", "ED40", "EA41", "ED41",
-    "EN50", "EN53", "EA51", "ED51", "ED43", "EA53", "ED53", "EA50", "ED50", "EN52", "EA52", "ED52",
-)
+EARLY_BANKS = ((0, 0), (0, 1), (0, 2), (1, 0), (1, 1), (1, 2), (2, 0), (2, 1))
+
+COPY_ENGINE = "VSVV" + "VSVSVSVSVSVS" + "SVSSVSSVSSVSSVSSVV"
+CQ_COPY_ENGINE = "SSSSVV"
+
+FIRST_ROPE_SLOT = (2, 0, 1)
+KV_ROPE_SLOT = 7
 
 
 def tile_mla_model_kernel(
@@ -54,426 +33,456 @@ def tile_mla_model_kernel(
 ):
     nc = tc.nc
     with ExitStack() as ctx:
-        if PINNED:
-            ctx.enter_context(tc.manual_schedule())
         const = ctx.enter_context(tc.tile_pool(name="const", bufs=1))
         keep = ctx.enter_context(tc.tile_pool(name="keep", bufs=1))
         raw_pool = ctx.enter_context(tc.tile_pool(name="raw", bufs=6))
-        wcp = ctx.enter_context(tc.tile_pool(name="wcp", bufs=6))
-        r4_pool = ctx.enter_context(tc.tile_pool(name="r4", bufs=5))
-        grp_pool = ctx.enter_context(tc.tile_pool(name="grp", bufs=6))
-        work = ctx.enter_context(tc.tile_pool(name="work", bufs=3))
-        junkp = ctx.enter_context(tc.tile_pool(name="junkp", bufs=2))
-        cgp = ctx.enter_context(tc.tile_pool(name="cgp", bufs=4))
-        cq_pool = ctx.enter_context(tc.tile_pool(name="cqp", bufs=3))
+        code_pool = ctx.enter_context(tc.tile_pool(name="codes", bufs=6))
+        small_raw = ctx.enter_context(tc.tile_pool(name="small_raw", bufs=5))
+        grouped_pool = ctx.enter_context(tc.tile_pool(name="grouped", bufs=6))
+        rope_pool = ctx.enter_context(tc.tile_pool(name="rope", bufs=3))
+        junk_pool = ctx.enter_context(tc.tile_pool(name="junk", bufs=2))
+        cqg_pool = ctx.enter_context(tc.tile_pool(name="cqg", bufs=4))
+        cq_pool = ctx.enter_context(tc.tile_pool(name="cq", bufs=3))
         stat = ctx.enter_context(tc.tile_pool(name="stat", bufs=4))
-        outp = ctx.enter_context(tc.tile_pool(name="outp", bufs=7))
+        out_pool = ctx.enter_context(tc.tile_pool(name="outp", bufs=7))
         psum = ctx.enter_context(tc.psum_pool(name="psum", bufs=8))
 
-        x_view = token_x.rearrange("(p t) h -> p t h", t=4)
-        out_view = out.rearrange("(p t) n -> p t n", t=4)
+        x_view = token_x.rearrange("(p t) h -> p t h", t=TILES)
+        out_view = out.rearrange("(p t) n -> p t n", t=TILES)
 
         eps = const.tile([P, 1], F32, name="eps")
         nc.vector.memset(eps[:], EPS)
-        zrow = grp_pool.tile([P, 2048], BF16, tag="grp", name="zrow", align_bytes=64)
-        nc.vector.memset(zrow[:], 0.0)
+        gain_rows = grouped_pool.tile([P, 4 * W], BF16, tag="grouped", name="gain_rows", align_bytes=64)
+        nc.vector.memset(gain_rows[:], 0.0)
         ones = const.tile([P, P], BF16, name="ones")
         nc.vector.memset(ones[:], 1.0)
-        cosb = const.tile([P, 4, DR], BF16, name="cosb")
-        sinb = const.tile([P, 4, DR], BF16, name="sinb")
+        cos_raw = const.tile([P, TILES, DR], BF16, name="cos_raw")
+        sin_raw = const.tile([P, TILES, DR], BF16, name="sin_raw")
         warm = const.tile([P, 1], F32, name="warm")
         nc.scalar.activation(out=warm[:], in_=eps[:], func=ACT.Sqrt)
-        ident_f = const.tile([P, P], F32, name="ident_f")
-        make_identity(nc, ident_f[:])
-        ident_b = const.tile([P, P], BF16, name="ident_b")
-        make_identity(nc, ident_b[:])
+        ident_f32 = const.tile([P, P], F32, name="ident_f32")
+        make_identity(nc, ident_f32[:])
+        ident_bf16 = const.tile([P, P], BF16, name="ident_bf16")
+        make_identity(nc, ident_bf16[:])
 
-        xr = []
-        rks = []
+        x_raw = []
+        wkv_raw = []
 
         def load_x(t, pieces):
-            xr.append(r4_pool.tile([P, H], BF16, tag="r4", name="xr%d" % t))
+            x_raw.append(small_raw.tile([P, H], BF16, tag="small", name="x_raw%d" % t))
             wid = H // pieces
             for i in range(pieces):
-                nc.sync.dma_start(out=xr[t][:, wid * i:wid * i + wid], in_=x_view[:, t, wid * i:wid * i + wid])
+                nc.sync.dma_start(out=x_raw[t][:, wid * i:wid * i + wid], in_=x_view[:, t, wid * i:wid * i + wid])
 
-        def load_k(g):
-            rk = r4_pool.tile([P, 4, 512], BF16, tag="r4", name="rk%d" % g)
+        def load_wkv(g):
+            chunk = small_raw.tile([P, 4, W], BF16, tag="small", name="wkv_raw%d" % g)
             nc.sync.dma_start(
-                out=rk[:].rearrange("p (u e) c -> p u e c", u=2),
+                out=chunk[:].rearrange("p (u e) c -> p u e c", u=2),
                 in_=wkv[512 * g:512 * g + 512, :].rearrange("(u q e) c -> q u e c", u=2, e=2),
             )
-            rks.append(rk)
+            wkv_raw.append(chunk)
 
-        for t in range(4):
-            load_x(t, 1)
-            load_k(t)
+        load_x(0, 2)
+        load_x(1, 1)
+        nc.sync.dma_start(out=gain_rows[0:1, 0:QR], in_=gamma_cq.unsqueeze(0))
+        nc.sync.dma_start(out=gain_rows[0:1, QR:QR + KVR], in_=gamma_ckv.unsqueeze(0))
+        nc.sync.dma_start(out=cos_raw[:], in_=rope_cos.rearrange("(p t) d -> p t d", t=TILES))
+        nc.sync.dma_start(out=sin_raw[:], in_=rope_sin.rearrange("(p t) d -> p t d", t=TILES))
+        load_wkv(0)
+        load_x(2, 1)
+        load_wkv(1)
+        load_x(3, 1)
+        load_wkv(2)
+        load_wkv(3)
 
+        table_1 = const.tile([P, TILES, DR], F32, name="table_1")
+        table_2 = const.tile([P, TILES, DR], F32, name="table_2")
+        nc.gpsimd.tensor_copy(out=table_1[:, :, 0:HALF], in_=cos_raw[:, :, 0:HALF])
+        nc.gpsimd.tensor_copy(out=table_1[:, :, HALF:DR], in_=sin_raw[:, :, HALF:DR])
+        nc.gpsimd.tensor_scalar(
+            out=table_2[:, :, 0:HALF], in0=sin_raw[:, :, 0:HALF], scalar1=-1.0, scalar2=0.0,
+            op0=ALU.mult, op1=ALU.add,
+        )
+        nc.gpsimd.tensor_copy(out=table_2[:, :, HALF:DR], in_=cos_raw[:, :, HALF:DR])
 
-        xc = keep.tile([P, 4, 512], U32, name="xc", align_bytes=64)
-        xs = keep.tile([P, 4, 512], U8, name="xs", align_bytes=64)
-        wk_c = keep.tile([P, 4, 512], U32, name="wk_c", align_bytes=64)
-        wk_s = keep.tile([P, 4, 512], U8, name="wk_s", align_bytes=64)
-        cqc = keep.tile([P, 4, 384], U32, name="cqc", align_bytes=64)
-        cqs = keep.tile([P, 4, 384], U8, name="cqs", align_bytes=64)
-        gam_q = const.tile([P, QR], BF16, name="gam_q")
-        gam_k = const.tile([P, 512], BF16, name="gam_k")
+        x_codes = keep.tile([P, TILES, W], U32, name="x_codes", align_bytes=64)
+        x_scales = keep.tile([P, TILES, W], U8, name="x_scales", align_bytes=64)
+        wkv_codes = keep.tile([P, 4, W], U32, name="wkv_codes", align_bytes=64)
+        wkv_scales = keep.tile([P, 4, W], U8, name="wkv_scales", align_bytes=64)
+        cq_codes = keep.tile([P, TILES, 3 * P], U32, name="cq_codes", align_bytes=64)
+        cq_scales = keep.tile([P, TILES, 3 * P], U8, name="cq_scales", align_bytes=64)
+        gain_q = const.tile([P, QR], BF16, name="gain_q")
+        gain_kv = const.tile([P, W], BF16, name="gain_kv")
 
         units = []
         for g in range(4):
-            units.append((rks[g][:], wk_c[:, g, :], wk_s[:, g, :], "V", ("K", g, 0)))
-        wa_c, wa_s = [], []
+            units.append((wkv_raw[g][:], wkv_codes[:, g, :], wkv_scales[:, g, :], None))
+        wa_codes, wa_scales = [], []
         for g in range(4):
-            rw = raw_pool.tile([P, 4, QR], BF16, tag="raw", name="rw%d" % g)
-            nc.sync.dma_start(
-                out=rw[:].rearrange("p (u e) c -> p u e c", u=2),
-                in_=wq_a[512 * g:512 * g + 512, :].rearrange("(u q e) c -> q u e c", u=2, e=2),
-            )
+            chunk = raw_pool.tile([P, 4, QR], BF16, tag="raw", name="wa_raw%d" % g)
             if g == 0:
-                nc.sync.dma_start(out=zrow[0:1, 0:QR], in_=gamma_cq.unsqueeze(0))
-                nc.sync.dma_start(out=zrow[0:1, QR:QR + KVR], in_=gamma_ckv.unsqueeze(0))
-                nc.sync.dma_start(out=cosb[:], in_=rope_cos.rearrange("(p t) d -> p t d", t=4))
-                nc.sync.dma_start(out=sinb[:], in_=rope_sin.rearrange("(p t) d -> p t d", t=4))
-            wa_c.append(wcp.tile([P, QR], U32, tag="wc", name="wa_c%d" % g, align_bytes=64))
-            wa_s.append(wcp.tile([P, QR], U8, tag="ws", name="wa_s%d" % g, align_bytes=64))
-            for c in range(3):
-                cols = slice(512 * c, 512 * c + 512)
-                units.append((rw[:, :, cols], wa_c[g][:, cols], wa_s[g][:, cols], ENG_A[3 * g + c], ("A", g, c)))
-        wb_c, wb_s = {}, {}
-        for hf in range(2):
-            rbs = []
-            for g in range(3):
-                rb = raw_pool.tile([P, 4, QR], BF16, tag="raw", name="rb%d%d" % (hf, g))
+                for c in range(3):
+                    for u in range(2):
+                        nc.sync.dma_start(
+                            out=chunk[:, 2 * u:2 * u + 2, W * c:W * c + W],
+                            in_=wq_a[256 * u:256 * u + 256, W * c:W * c + W].rearrange("(q e) c -> q e c", e=2),
+                        )
+            else:
                 nc.sync.dma_start(
-                    out=rb[:],
-                    in_=wq_b[512 * g:512 * g + 512, QR * hf:QR * hf + QR].rearrange("(j p) n -> p j n", p=P),
+                    out=chunk[:].rearrange("p (u e) c -> p u e c", u=2),
+                    in_=wq_a[512 * g:512 * g + 512, :].rearrange("(u q e) c -> q u e c", u=2, e=2),
                 )
-                rbs.append(rb)
-                wb_c[(hf, g)] = wcp.tile([P, QR], U32, tag="wc", name="wb_c%d%d" % (hf, g), align_bytes=64)
-                wb_s[(hf, g)] = wcp.tile([P, QR], U8, tag="ws", name="wb_s%d%d" % (hf, g), align_bytes=64)
+            wa_codes.append(code_pool.tile([P, QR], U32, tag="codes", name="wa_codes%d" % g, align_bytes=64))
+            wa_scales.append(code_pool.tile([P, QR], U8, tag="scales", name="wa_scales%d" % g, align_bytes=64))
             for c in range(3):
-                cols = slice(512 * c, 512 * c + 512)
+                cols = slice(W * c, W * c + W)
+                units.append((chunk[:, :, cols], wa_codes[g][:, cols], wa_scales[g][:, cols], ("a", g, c)))
+        wb_codes, wb_scales = {}, {}
+        for half in range(2):
+            chunks = []
+            for g in range(3):
+                chunk = raw_pool.tile([P, 4, QR], BF16, tag="raw", name="wb_raw%d%d" % (half, g))
+                nc.sync.dma_start(
+                    out=chunk[:],
+                    in_=wq_b[512 * g:512 * g + 512, QR * half:QR * half + QR].rearrange("(j p) n -> p j n", p=P),
+                )
+                chunks.append(chunk)
+                wb_codes[(half, g)] = code_pool.tile(
+                    [P, QR], U32, tag="codes", name="wb_codes%d%d" % (half, g), align_bytes=64
+                )
+                wb_scales[(half, g)] = code_pool.tile(
+                    [P, QR], U8, tag="scales", name="wb_scales%d%d" % (half, g), align_bytes=64
+                )
+            for c in range(3):
+                cols = slice(W * c, W * c + W)
                 for g in range(3):
                     units.append((
-                        rbs[g][:, :, cols], wb_c[(hf, g)][:, cols], wb_s[(hf, g)][:, cols],
-                        ENG_B[9 * hf + 3 * c + g], ("B", 3 * hf + c, g),
+                        chunks[g][:, :, cols], wb_codes[(half, g)][:, cols], wb_scales[(half, g)][:, cols],
+                        ("q", 3 * half + c, g),
                     ))
-
-        tab_a = const.tile([P, 4, DR], F32, name="tab_a")
-        tab_b = const.tile([P, 4, DR], F32, name="tab_b")
-        nc.gpsimd.tensor_copy(out=tab_a[:, :, 0:32], in_=cosb[:, :, 0:32])
-        nc.gpsimd.tensor_copy(out=tab_a[:, :, 32:64], in_=sinb[:, :, 32:64])
-        nc.gpsimd.tensor_scalar(
-            out=tab_b[:, :, 0:32], in0=sinb[:, :, 0:32], scalar1=-1.0, scalar2=0.0,
-            op0=ALU.mult, op1=ALU.add,
-        )
-        nc.gpsimd.tensor_copy(out=tab_b[:, :, 32:64], in_=cosb[:, :, 32:64])
 
         a_bank = {}
         q_bank = {}
         grouped = {}
-        pos = {"r": 0, "z": 0, "m": 0}
+        done = {"copied": 0, "quantised": 0, "multiplied": 0}
 
         def stage1_pass(t, c, g):
-            cols = slice(512 * c, 512 * c + 512)
+            cols = slice(W * c, W * c + W)
             nc.tensor.matmul_mx(
                 out=a_bank[(t, c)][:],
-                lhsT=xc[:, t, P * g:P * g + P].bitcast(FP8X4),
-                lhsT_scale=xs[:, t, P * g:P * g + P],
-                rhs=wa_c[g][:, cols].bitcast(FP8X4),
-                rhs_scale=wa_s[g][:, cols],
+                lhsT=x_codes[:, t, P * g:P * g + P].bitcast(FP8X4),
+                lhsT_scale=x_scales[:, t, P * g:P * g + P],
+                rhs=wa_codes[g][:, cols].bitcast(FP8X4),
+                rhs_scale=wa_scales[g][:, cols],
                 start=(g == 0),
                 stop=(g == 3),
             )
 
-        def passes_after(what):
-            kind, i, j = what
-            if kind == "A":
-                g, c = i, j
-                for t in range(4):
-                    if (t, c) in STREAM:
+        def regroup_next():
+            k = done["copied"]
+            if k >= len(units):
+                return
+            done["copied"] = k + 1
+            grouped[k] = grouped_pool.tile([P, 4 * W], BF16, tag="grouped", name="grouped%d" % k, align_bytes=64)
+            dst = grouped[k][:].rearrange("p (c i t) -> p c t i", i=4, t=4)
+            src = units[k][0].rearrange("p t (c i) -> p c t i", i=4)
+            if COPY_ENGINE[k] == "S":
+                nc.scalar.copy(out=dst, in_=src)
+            else:
+                nc.vector.tensor_copy(out=dst, in_=src)
+
+        def quantise_next():
+            k = done["quantised"]
+            if k >= len(units):
+                return
+            done["quantised"] = k + 1
+            nc.vector.quantize_mx(out=units[k][1].bitcast(FP8X4), scales=units[k][2], in_=grouped[k][:])
+
+        def multiply_next():
+            k = done["multiplied"]
+            if k >= len(units):
+                return
+            done["multiplied"] = k + 1
+            what = units[k][3]
+            if what is None:
+                return
+            if what[0] == "a":
+                g, c = what[1], what[2]
+                for t in range(TILES):
+                    if (t, c) in EARLY_BANKS:
                         if g == 0:
-                            a_bank[(t, c)] = psum.tile([P, 512], F32, tag="bank", name="a%d%d" % (t, c))
+                            a_bank[(t, c)] = psum.tile([P, W], F32, tag="bank", name="a%d%d" % (t, c))
                         stage1_pass(t, c, g)
-            if kind == "B":
-                s, g = i, j
-                hf, c = divmod(s, 3)
-                cols = slice(512 * c, 512 * c + 512)
-                for t in range(4):
+            else:
+                s, g = what[1], what[2]
+                half, c = divmod(s, 3)
+                cols = slice(W * c, W * c + W)
+                for t in range(TILES):
                     if g == 0:
-                        q_bank[(s, t)] = psum.tile([P, 512], F32, tag="bank", name="q%d%d" % (s, t))
+                        q_bank[(s, t)] = psum.tile([P, W], F32, tag="bank", name="q%d%d" % (s, t))
                     nc.tensor.matmul_mx(
                         out=q_bank[(s, t)][:],
-                        lhsT=cqc[:, t, P * g:P * g + P].bitcast(FP8X4),
-                        lhsT_scale=cqs[:, t, P * g:P * g + P],
-                        rhs=wb_c[(hf, g)][:, cols].bitcast(FP8X4),
-                        rhs_scale=wb_s[(hf, g)][:, cols],
+                        lhsT=cq_codes[:, t, P * g:P * g + P].bitcast(FP8X4),
+                        lhsT_scale=cq_scales[:, t, P * g:P * g + P],
+                        rhs=wb_codes[(half, g)][:, cols].bitcast(FP8X4),
+                        rhs_scale=wb_scales[(half, g)][:, cols],
                         start=(g == 0),
                         stop=(g == 2),
                     )
 
-        def regroup_next(eng):
-            k = pos["r"]
-            if k >= len(units):
-                return
-            pos["r"] = k + 1
-            src, codes, scales, unused, what = units[k]
-            wg = grp_pool.tile([P, 2048], BF16, tag="grp", name="wg%d" % k, align_bytes=64)
-            grouped[k] = wg
-            dst = wg[:].rearrange("p (c i t) -> p c t i", i=4, t=4)
-            view = src.rearrange("p t (c i) -> p c t i", i=4)
-            if eng == "S":
-                nc.scalar.copy(out=dst, in_=view)
-            else:
-                nc.vector.tensor_copy(out=dst, in_=view)
+        def advance():
+            regroup_next()
+            quantise_next()
+            multiply_next()
 
-        def quantise_next():
-            k = pos["z"]
-            if k >= len(units):
-                return
-            pos["z"] = k + 1
-            src, codes, scales, eng, what = units[k]
-            nc.vector.quantize_mx(out=codes.bitcast(FP8X4), scales=scales, in_=grouped[k][:])
-
-        def passes_next():
-            k = pos["m"]
-            assert k < pos["z"]
-            pos["m"] = k + 1
-            passes_after(units[k][4])
-
-        xg = {}
-
-        xts = {}
+        x_grouped = {}
+        x_bank = {}
 
         def x_transpose(t):
-            x32 = xr[t][:].bitcast(F32)
-            xg[t] = grp_pool.tile([P, 2048], BF16, tag="grp", name="xg%d" % t, align_bytes=64)
-            for gp in range(2):
-                xt = psum.tile([P, 4, P], F32, tag="bank", name="xt%d%d" % (t, gp))
-                xts[(t, gp)] = xt
+            words = x_raw[t][:].bitcast(F32)
+            x_grouped[t] = grouped_pool.tile([P, 4 * W], BF16, tag="grouped", name="x_grouped%d" % t, align_bytes=64)
+            for pair in range(2):
+                x_bank[(t, pair)] = psum.tile([P, 4, P], F32, tag="bank", name="x_bank%d%d" % (t, pair))
                 for i in range(4):
-                    w0 = 512 * gp + P * i
-                    nc.tensor.transpose(out=xt[:, i, :], in_=x32[:, w0:w0 + P], identity=ident_f[:])
-
-        def x_copy(t, gp, eng):
-            xg32 = xg[t][:].bitcast(F32)
-            dst = xg32[:, 512 * gp:512 * gp + 512].rearrange("p (g r u) -> p g r u", g=2, u=2)
-            view = xts[(t, gp)][:].rearrange("p (g u) r -> p g r u", u=2)
-            if eng == "S":
-                nc.scalar.copy(out=dst, in_=view)
-            else:
-                nc.vector.tensor_copy(out=dst, in_=view)
+                    w0 = W * pair + P * i
+                    nc.tensor.transpose(out=x_bank[(t, pair)][:, i, :], in_=words[:, w0:w0 + P], identity=ident_f32[:])
+            for pair in range(2):
+                dst = x_grouped[t][:].bitcast(F32)[:, W * pair:W * pair + W].rearrange("p (g r u) -> p g r u", g=2, u=2)
+                nc.scalar.copy(out=dst, in_=x_bank[(t, pair)][:].rearrange("p (g u) r -> p g r u", u=2))
 
         def x_quantise(t):
-            nc.vector.quantize_mx(out=xc[:, t, :].bitcast(FP8X4), scales=xs[:, t, :], in_=xg[t][:])
+            nc.vector.quantize_mx(out=x_codes[:, t, :].bitcast(FP8X4), scales=x_scales[:, t, :], in_=x_grouped[t][:])
 
         def spread_gains(c):
-            gb = psum.tile([P, 512], F32, tag="bank", name="gb%d" % c)
-            nc.tensor.matmul(out=gb[:], lhsT=ones[:], rhs=zrow[:, 512 * c:512 * c + 512], start=True, stop=True)
+            bank = psum.tile([P, W], F32, tag="bank", name="gain_bank%d" % c)
+            nc.tensor.matmul(out=bank[:], lhsT=ones[:], rhs=gain_rows[:, W * c:W * c + W], start=True, stop=True)
             if c < 3:
-                nc.scalar.copy(out=gam_q[:, 512 * c:512 * c + 512], in_=gb[:])
+                nc.scalar.copy(out=gain_q[:, W * c:W * c + W], in_=bank[:])
             else:
-                nc.scalar.copy(out=gam_k[:], in_=gb[:])
+                nc.scalar.copy(out=gain_kv[:], in_=bank[:])
 
-
-        cq_tiles = {}
-        ssq = {}
-        rstd = {}
+        cq = {}
+        sums = {}
         rms = {}
+        cq_bank = {}
+        cq_grouped = {}
+        cq_codes_flat = cq_codes[:].rearrange("p t w -> p (t w)")
+        cq_scales_flat = cq_scales[:].rearrange("p t w -> p (t w)")
 
-        def squares(t, cs):
-            if t not in ssq:
-                ssq[t] = stat.tile([P, 4], F32, tag="ssq", name="ssq%d" % t)
-            for c in cs:
-                junk = junkp.tile([P, 512], BF16, tag="junk", name="junk")
+        def squares(t, thirds):
+            if t not in sums:
+                sums[t] = stat.tile([P, 4], F32, tag="sums", name="sums%d" % t)
+            for c in thirds:
+                junk = junk_pool.tile([P, W], BF16, tag="junk", name="junk")
                 nc.scalar.activation(
-                    out=junk[:], in_=a_bank[(t, c)][:], func=ACT.Square, accum_out=ssq[t][:, c:c + 1]
+                    out=junk[:], in_=a_bank[(t, c)][:], func=ACT.Square, accum_out=sums[t][:, c:c + 1]
                 )
 
-        def stats(t):
-            ss = stat.tile([P, 1], F32, tag="ss", name="ss%d" % t)
-            j3 = stat.tile([P, 4], F32, tag="j3", name="j3")
-            nc.scalar.activation(out=j3[:, 0:3], in_=ssq[t][:, 0:3], func=ACT.Copy, accum_out=ss[:])
+        def root_mean_square(t):
+            total = stat.tile([P, 1], F32, tag="total", name="total%d" % t)
+            copy3 = stat.tile([P, 4], F32, tag="copy3", name="copy3")
+            nc.scalar.activation(out=copy3[:, 0:3], in_=sums[t][:, 0:3], func=ACT.Copy, accum_out=total[:])
             rms[t] = stat.tile([P, 1], F32, tag="rms", name="rms%d" % t)
-            nc.scalar.activation(out=rms[t][:], in_=ss[:], func=ACT.Sqrt, bias=eps[:, 0:1], scale=1.0 / QR)
+            nc.scalar.activation(out=rms[t][:], in_=total[:], func=ACT.Sqrt, bias=eps[:, 0:1], scale=1.0 / QR)
 
         def scale_cq(t):
-            rstd[t] = stat.tile([P, 1], F32, tag="rstd", name="rstd%d" % t)
-            nc.vector.reciprocal(out=rstd[t][:], in_=rms[t][:])
-            cq = cq_pool.tile([P, QR], BF16, tag="cq", name="cq%d" % t)
+            rstd = stat.tile([P, 1], F32, tag="rstd", name="rstd%d" % t)
+            nc.vector.reciprocal(out=rstd[:], in_=rms[t][:])
+            cq[t] = cq_pool.tile([P, QR], BF16, tag="cq", name="cq%d" % t)
             for c in range(3):
-                cols = slice(512 * c, 512 * c + 512)
+                cols = slice(W * c, W * c + W)
                 nc.vector.scalar_tensor_tensor(
-                    out=cq[:, cols], in0=a_bank[(t, c)][:], scalar=rstd[t][:, 0:1], in1=gam_q[:, cols],
+                    out=cq[t][:, cols], in0=a_bank[(t, c)][:], scalar=rstd[:, 0:1], in1=gain_q[:, cols],
                     op0=ALU.mult, op1=ALU.mult,
                 )
-            cq_tiles[t] = cq
 
-        cgs = {}
-        tps = {}
-        cqc_flat = cqc[:].rearrange("p t w -> p (t w)")
-        cqs_flat = cqs[:].rearrange("p t w -> p (t w)")
+        def late_bank(t, c):
+            a_bank[(t, c)] = psum.tile([P, W], F32, tag="bank", name="a%d%d" % (t, c))
+            for g in range(4):
+                stage1_pass(t, c, g)
 
         def cq_transpose(pair):
-            tp = psum.tile([P, 8, P], BF16, tag="bank", name="tp%d" % pair)
-            tps[pair] = tp
+            cq_bank[pair] = psum.tile([P, 8, P], BF16, tag="bank", name="cq_bank%d" % pair)
             for h in range(2):
                 t, g = divmod(2 * pair + h, 3)
                 for j in range(4):
                     k0 = 512 * g + P * j
-                    nc.tensor.transpose(out=tp[:, 4 * h + j, :], in_=cq_tiles[t][:, k0:k0 + P], identity=ident_b[:])
+                    nc.tensor.transpose(
+                        out=cq_bank[pair][:, 4 * h + j, :], in_=cq[t][:, k0:k0 + P], identity=ident_bf16[:]
+                    )
 
-        def cq_copy(pair, eng):
-            cg = cgp.tile([P, 1024], BF16, tag="cg", name="cg%d" % pair, align_bytes=64)
-            cgs[pair] = cg
-            dst = cg[:].rearrange("p (h r j) -> p h r j", h=2, j=4)
-            view = tps[pair][:].rearrange("p (h j) r -> p h r j", h=2)
-            if eng == "S":
-                nc.scalar.copy(out=dst, in_=view)
+        def cq_copy(pair):
+            cq_grouped[pair] = cqg_pool.tile([P, 2 * W], BF16, tag="cqg", name="cq_grouped%d" % pair, align_bytes=64)
+            dst = cq_grouped[pair][:].rearrange("p (h r j) -> p h r j", h=2, j=4)
+            src = cq_bank[pair][:].rearrange("p (h j) r -> p h r j", h=2)
+            if CQ_COPY_ENGINE[pair] == "S":
+                nc.scalar.copy(out=dst, in_=src)
             else:
-                nc.vector.tensor_copy(out=dst, in_=view)
+                nc.vector.tensor_copy(out=dst, in_=src)
 
         def cq_quantise(pair):
             nc.vector.quantize_mx(
-                out=cqc_flat[:, 256 * pair:256 * pair + 256].bitcast(FP8X4),
-                scales=cqs_flat[:, 256 * pair:256 * pair + 256],
-                in_=cgs[pair][:],
+                out=cq_codes_flat[:, 2 * P * pair:2 * P * pair + 2 * P].bitcast(FP8X4),
+                scales=cq_scales_flat[:, 2 * P * pair:2 * P * pair + 2 * P],
+                in_=cq_grouped[pair][:],
             )
 
-        def late_bank(t, c):
-            a_bank[(t, c)] = psum.tile([P, 512], F32, tag="bank", name="a%d%d" % (t, c))
-            for g in range(4):
-                stage1_pass(t, c, g)
+        products = {}
+        out_tile = {}
 
-        prod = {}
+        def rope_products(key, bank, first_slot, t):
+            n = len(range(first_slot, 8, 3))
+            halves = bank[:].rearrange("p (s w) -> p s w", w=HALF)
+            shape = [P, n, 2, HALF]
+            x1 = halves[:, 2 * first_slot:16:6, :].unsqueeze(2).to_broadcast(shape)
+            x2 = halves[:, 2 * first_slot + 1:16:6, :].unsqueeze(2).to_broadcast(shape)
+            t1 = table_1[:, t, :].rearrange("p (h w) -> p h w", h=2).unsqueeze(1).to_broadcast(shape)
+            t2 = table_2[:, t, :].rearrange("p (h w) -> p h w", h=2).unsqueeze(1).to_broadcast(shape)
+            p1 = rope_pool.tile([P, 3, 2, HALF], F32, tag="p1", name="p1")
+            p2 = rope_pool.tile([P, 3, 2, HALF], F32, tag="p2", name="p2")
+            nc.vector.tensor_tensor(out=p1[:, 0:n], in0=x1, in1=t1, op=ALU.mult)
+            nc.vector.tensor_tensor(out=p2[:, 0:n], in0=x2, in1=t2, op=ALU.mult)
+            products[key] = (p1, p2, n, first_slot)
 
-        def rope_products(key, bank, s0, t):
-            nb = len(range(s0, 8, 3))
-            b32 = bank[:].rearrange("p (s w) -> p s w", w=32)
-            shape = [P, nb, 2, 32]
-            x1 = b32[:, 2 * s0:16:6, :].unsqueeze(2).to_broadcast(shape)
-            x2 = b32[:, 2 * s0 + 1:16:6, :].unsqueeze(2).to_broadcast(shape)
-            ta = tab_a[:, t, :].rearrange("p (h w) -> p h w", h=2).unsqueeze(1).to_broadcast(shape)
-            tb = tab_b[:, t, :].rearrange("p (h w) -> p h w", h=2).unsqueeze(1).to_broadcast(shape)
-            pa = work.tile([P, 3, 2, 32], F32, tag="pa", name="pa")
-            pb = work.tile([P, 3, 2, 32], F32, tag="pb", name="pb")
-            nc.vector.tensor_tensor(out=pa[:, 0:nb], in0=x1, in1=ta, op=ALU.mult)
-            nc.vector.tensor_tensor(out=pb[:, 0:nb], in0=x2, in1=tb, op=ALU.mult)
-            prod[key] = (pa, pb, nb, s0)
-
-        def rope_sum(key, ot):
-            pa, pb, nb, s0 = prod[key]
-            o64 = ot[:].rearrange("p (s h w) -> p s h w", h=2, w=32)
-            nc.vector.tensor_tensor(out=o64[:, s0:8:3], in0=pa[:, 0:nb], in1=pb[:, 0:nb], op=ALU.add)
+        def rope_sum(key):
+            p1, p2, n, first_slot = products[key]
+            slots = out_tile[key][:].rearrange("p (s h w) -> p s h w", h=2, w=HALF)
+            nc.vector.tensor_tensor(out=slots[:, first_slot:8:3], in0=p1[:, 0:n], in1=p2[:, 0:n], op=ALU.add)
 
         kv_bank = {}
-        ots = {}
-        rsk = {}
-        rmk = {}
+        kv_rms = {}
 
         def kv_passes(t):
-            kv_bank[t] = psum.tile([P, 512], F32, tag="bank", name="kv%d" % t)
+            kv_bank[t] = psum.tile([P, W], F32, tag="bank", name="kv%d" % t)
             for g in range(4):
                 nc.tensor.matmul_mx(
                     out=kv_bank[t][:],
-                    lhsT=xc[:, t, P * g:P * g + P].bitcast(FP8X4),
-                    lhsT_scale=xs[:, t, P * g:P * g + P],
-                    rhs=wk_c[:, g, :].bitcast(FP8X4),
-                    rhs_scale=wk_s[:, g, :],
+                    lhsT=x_codes[:, t, P * g:P * g + P].bitcast(FP8X4),
+                    lhsT_scale=x_scales[:, t, P * g:P * g + P],
+                    rhs=wkv_codes[:, g, :].bitcast(FP8X4),
+                    rhs_scale=wkv_scales[:, g, :],
                     start=(g == 0),
                     stop=(g == 3),
                 )
 
-        def kv_stats(t):
-            ssk = stat.tile([P, 1], F32, tag="ss", name="ssk%d" % t)
-            junk = junkp.tile([P, 512], BF16, tag="junk", name="junk")
-            nc.scalar.activation(
-                out=junk[:, 0:KVR], in_=kv_bank[t][:, 0:KVR], func=ACT.Square, accum_out=ssk[:]
-            )
-            rmk[t] = stat.tile([P, 1], F32, tag="rms", name="rmk%d" % t)
-            nc.scalar.activation(out=rmk[t][:], in_=ssk[:], func=ACT.Sqrt, bias=eps[:, 0:1], scale=1.0 / KVR)
+        def kv_root_mean_square(t):
+            total = stat.tile([P, 1], F32, tag="total", name="kv_total%d" % t)
+            junk = junk_pool.tile([P, W], BF16, tag="junk", name="junk")
+            nc.scalar.activation(out=junk[:, 0:KVR], in_=kv_bank[t][:, 0:KVR], func=ACT.Square, accum_out=total[:])
+            kv_rms[t] = stat.tile([P, 1], F32, tag="rms", name="kv_rms%d" % t)
+            nc.scalar.activation(out=kv_rms[t][:], in_=total[:], func=ACT.Sqrt, bias=eps[:, 0:1], scale=1.0 / KVR)
 
         def kv_finish(t):
-            rsk[t] = stat.tile([P, 1], F32, tag="rstd", name="rsk%d" % t)
-            nc.vector.reciprocal(out=rsk[t][:], in_=rmk[t][:])
-            ot = outp.tile([P, 512], F32, tag="ot", name="otk%d" % t)
+            rstd = stat.tile([P, 1], F32, tag="rstd", name="kv_rstd%d" % t)
+            nc.vector.reciprocal(out=rstd[:], in_=kv_rms[t][:])
+            out_tile[("kv", t)] = out_pool.tile([P, W], F32, tag="out", name="kv_out%d" % t)
             nc.vector.scalar_tensor_tensor(
-                out=ot[:, 0:KVR], in0=kv_bank[t][:, 0:KVR], scalar=rsk[t][:, 0:1], in1=gam_k[:, 0:KVR],
-                op0=ALU.mult, op1=ALU.mult,
+                out=out_tile[("kv", t)][:, 0:KVR], in0=kv_bank[t][:, 0:KVR], scalar=rstd[:, 0:1],
+                in1=gain_kv[:, 0:KVR], op0=ALU.mult, op1=ALU.mult,
             )
-            rope_products(("k", t), kv_bank[t], 7, t)
-            ots[("k", t)] = ot
+            rope_products(("kv", t), kv_bank[t], KV_ROPE_SLOT, t)
+            rope_sum(("kv", t))
+            nc.sync.dma_start(out=out_view[:, t, NQ:NQ + KV], in_=out_tile[("kv", t)][:])
 
-        def kv_store(t):
-            rope_sum(("k", t), ots[("k", t)])
-            nc.sync.dma_start(out=out_view[:, t, NQ:NQ + KV], in_=ots[("k", t)][:])
-
-        def nope_out(s, t):
-            s0 = ROPE_SLOT[s % 3]
-            ot = outp.tile([P, 512], F32, tag="ot", name="ot%d%d" % (s, t))
-            ots[(s, t)] = ot
-            q64 = q_bank[(s, t)][:].rearrange("p (s w) -> p s w", w=64)
-            o64 = ot[:].rearrange("p (s w) -> p s w", w=64)
+        def plain_columns_out(s, t):
+            rope_class = FIRST_ROPE_SLOT[s % 3] % 3
+            out_tile[(s, t)] = out_pool.tile([P, W], F32, tag="out", name="q_out%d%d" % (s, t))
+            src = q_bank[(s, t)][:].rearrange("p (s w) -> p s w", w=DR)
+            dst = out_tile[(s, t)][:].rearrange("p (s w) -> p s w", w=DR)
             for r in range(3):
-                if r != s0 % 3:
-                    nc.scalar.copy(out=o64[:, r:8:3, :], in_=q64[:, r:8:3, :])
+                if r != rope_class:
+                    nc.scalar.copy(out=dst[:, r:8:3, :], in_=src[:, r:8:3, :])
 
-        def store(s, t):
-            rope_sum((s, t), ots[(s, t)])
-            nc.sync.dma_start(out=out_view[:, t, 512 * s:512 * s + 512], in_=ots[(s, t)][:])
+        def q_store(s, t):
+            rope_sum((s, t))
+            nc.sync.dma_start(out=out_view[:, t, W * s:W * s + W], in_=out_tile[(s, t)][:])
 
-        def run(tok):
-            op, a = tok[:2], [int(ch) for ch in tok[2:] if ch in "0123456789"]
-            if op == "RV":
-                regroup_next("V")
-            elif op == "RS":
-                regroup_next("S")
-            elif op == "ZZ":
-                quantise_next()
-            elif op == "XP":
-                x_transpose(a[0])
-            elif op == "XC":
-                x_copy(a[0], a[1], "S")
-            elif op == "XD":
-                x_copy(a[0], a[1], "V")
-            elif op == "XZ":
-                x_quantise(a[0])
-            elif op == "GB":
-                spread_gains(a[0])
-            elif op == "MM":
-                passes_next()
-            elif op == "SQ":
-                squares(a[0], (a[1],))
-            elif op == "ST":
-                stats(a[0])
-            elif op == "SC":
-                scale_cq(a[0])
-            elif op == "LB":
-                late_bank(a[0], a[1])
-            elif op == "TT":
-                cq_transpose(a[0])
-            elif op == "CV":
-                cq_copy(a[0], "V")
-            elif op == "CS":
-                cq_copy(a[0], "S")
-            elif op == "TZ":
-                cq_quantise(a[0])
-            elif op == "KM":
-                kv_passes(a[0])
-            elif op == "KS":
-                kv_stats(a[0])
-            elif op == "KF":
-                kv_finish(a[0])
-            elif op == "KD":
-                kv_store(a[0])
-            elif op == "EN":
-                nope_out(a[0], a[1])
-            elif op == "EA":
-                rope_products((a[0], a[1]), q_bank[(a[0], a[1])], ROPE_SLOT[a[0] % 3], a[1])
-            elif op == "ED":
-                store(a[0], a[1])
-            else:
-                raise ValueError(tok)
+        x_transpose(0)
+        x_transpose(1)
+        x_quantise(0)
+        regroup_next()
+        x_transpose(2)
+        x_quantise(1)
+        regroup_next()
+        quantise_next()
+        multiply_next()
+        x_transpose(3)
+        x_quantise(2)
+        advance()
+        x_quantise(3)
+        for c in (3, 0, 1, 2):
+            spread_gains(c)
+        advance()
+        advance()
+        for t in range(TILES):
+            kv_passes(t)
+        advance()
+        kv_root_mean_square(0)
+        kv_root_mean_square(1)
+        advance()
+        kv_root_mean_square(2)
+        kv_finish(0)
+        advance()
+        kv_root_mean_square(3)
+        kv_finish(1)
+        advance()
+        kv_finish(2)
+        advance()
+        kv_finish(3)
 
-        for tok in SEQ:
-            run(tok)
+        regroup_next()
+        for k in range(7):
+            advance()
+
+        squares(0, (0, 1, 2))
+        root_mean_square(0)
+        quantise_next()
+        squares(1, (0, 1, 2))
+        root_mean_square(1)
+        scale_cq(0)
+        late_bank(2, 2)
+        late_bank(3, 0)
+        late_bank(3, 1)
+        squares(2, (0, 1))
+        scale_cq(1)
+        late_bank(3, 2)
+        squares(2, (2,))
+        root_mean_square(2)
+        cq_transpose(0)
+        squares(3, (0,))
+        scale_cq(2)
+        squares(3, (1, 2))
+        root_mean_square(3)
+        cq_transpose(1)
+        cq_transpose(2)
+        cq_copy(0)
+        scale_cq(3)
+        cq_transpose(3)
+        cq_copy(1)
+        cq_quantise(0)
+        cq_transpose(4)
+        cq_transpose(5)
+        cq_copy(2)
+        cq_copy(4)
+        cq_quantise(1)
+        cq_copy(3)
+        cq_copy(5)
+        cq_quantise(2)
+        cq_quantise(4)
+        cq_quantise(3)
+        cq_quantise(5)
+        multiply_next()
+        advance()
+        advance()
+
+        banks = [(s, t) for s in range(6) for t in range(TILES)]
+        for n in range(len(banks) + 2):
+            if n < len(banks):
+                plain_columns_out(*banks[n])
+            if 1 <= n <= len(banks):
+                s, t = banks[n - 1]
+                rope_products((s, t), q_bank[(s, t)], FIRST_ROPE_SLOT[s % 3], t)
+            if n >= 2:
+                q_store(*banks[n - 2])
+            if n % 4 != 3:
+                advance()

from contextlib import ExitStack

import concourse.mybir as mybir
from concourse.masks import make_identity

F32 = mybir.dt.float32
BF16 = mybir.dt.bfloat16
U32 = mybir.dt.uint32
U8 = mybir.dt.uint8
FP8X4 = mybir.dt.float8_e4m3fn_x4
ALU = mybir.AluOpType
ACT = mybir.ActivationFunctionType

P = 128
TILES = 4
T, H, QR, NQ, KV, KVR, DR = 512, 2048, 1536, 3072, 512, 448, 64
HALF = DR // 2
W = 512
EPS = 1e-6
FLOPS = 2 * T * (H * QR + QR * NQ + H * KV)

EARLY_BANKS = ((0, 0), (0, 1), (0, 2), (1, 0), (1, 1), (1, 2), (2, 0), (2, 1))

COPY_ENGINE = "VSVV" + "VSVSVSVSVSVS" + "SVSSVSSVSSVSSVSSVV"
CQ_COPY_ENGINE = "SSSSVV"

FIRST_ROPE_SLOT = (2, 0, 1)
KV_ROPE_SLOT = 7


def tile_mla_model_kernel(
    tc, token_x, wq_a, wq_b, wkv, rope_cos, rope_sin, gamma_cq, gamma_ckv, out
):
    nc = tc.nc
    with ExitStack() as ctx:
        const = ctx.enter_context(tc.tile_pool(name="const", bufs=1))
        keep = ctx.enter_context(tc.tile_pool(name="keep", bufs=1))
        raw_pool = ctx.enter_context(tc.tile_pool(name="raw", bufs=6))
        code_pool = ctx.enter_context(tc.tile_pool(name="codes", bufs=6))
        small_raw = ctx.enter_context(tc.tile_pool(name="small_raw", bufs=5))
        grouped_pool = ctx.enter_context(tc.tile_pool(name="grouped", bufs=6))
        rope_pool = ctx.enter_context(tc.tile_pool(name="rope", bufs=3))
        junk_pool = ctx.enter_context(tc.tile_pool(name="junk", bufs=2))
        cqg_pool = ctx.enter_context(tc.tile_pool(name="cqg", bufs=4))
        cq_pool = ctx.enter_context(tc.tile_pool(name="cq", bufs=3))
        stat = ctx.enter_context(tc.tile_pool(name="stat", bufs=4))
        out_pool = ctx.enter_context(tc.tile_pool(name="outp", bufs=7))
        psum = ctx.enter_context(tc.psum_pool(name="psum", bufs=8))

        x_view = token_x.rearrange("(p t) h -> p t h", t=TILES)
        out_view = out.rearrange("(p t) n -> p t n", t=TILES)

        eps = const.tile([P, 1], F32, name="eps")
        nc.vector.memset(eps[:], EPS)
        gain_rows = grouped_pool.tile([P, 4 * W], BF16, tag="grouped", name="gain_rows", align_bytes=64)
        nc.vector.memset(gain_rows[:], 0.0)
        ones = const.tile([P, P], BF16, name="ones")
        nc.vector.memset(ones[:], 1.0)
        cos_raw = const.tile([P, TILES, DR], BF16, name="cos_raw")
        sin_raw = const.tile([P, TILES, DR], BF16, name="sin_raw")
        warm = const.tile([P, 1], F32, name="warm")
        nc.scalar.activation(out=warm[:], in_=eps[:], func=ACT.Sqrt)
        ident_f32 = const.tile([P, P], F32, name="ident_f32")
        make_identity(nc, ident_f32[:])
        ident_bf16 = const.tile([P, P], BF16, name="ident_bf16")
        make_identity(nc, ident_bf16[:])

        x_raw = []
        wkv_raw = []

        def load_x(t, pieces):
            x_raw.append(small_raw.tile([P, H], BF16, tag="small", name="x_raw%d" % t))
            wid = H // pieces
            for i in range(pieces):
                nc.sync.dma_start(out=x_raw[t][:, wid * i:wid * i + wid], in_=x_view[:, t, wid * i:wid * i + wid])

        def load_wkv(g):
            chunk = small_raw.tile([P, 4, W], BF16, tag="small", name="wkv_raw%d" % g)
            nc.sync.dma_start(
                out=chunk[:].rearrange("p (u e) c -> p u e c", u=2),
                in_=wkv[512 * g:512 * g + 512, :].rearrange("(u q e) c -> q u e c", u=2, e=2),
            )
            wkv_raw.append(chunk)

        load_x(0, 2)
        load_x(1, 1)
        nc.sync.dma_start(out=gain_rows[0:1, 0:QR], in_=gamma_cq.unsqueeze(0))
        nc.sync.dma_start(out=gain_rows[0:1, QR:QR + KVR], in_=gamma_ckv.unsqueeze(0))
        nc.sync.dma_start(out=cos_raw[:], in_=rope_cos.rearrange("(p t) d -> p t d", t=TILES))
        nc.sync.dma_start(out=sin_raw[:], in_=rope_sin.rearrange("(p t) d -> p t d", t=TILES))
        load_wkv(0)
        load_x(2, 1)
        load_wkv(1)
        load_x(3, 1)
        load_wkv(2)
        load_wkv(3)

        table_1 = const.tile([P, TILES, DR], F32, name="table_1")
        table_2 = const.tile([P, TILES, DR], F32, name="table_2")
        nc.gpsimd.tensor_copy(out=table_1[:, :, 0:HALF], in_=cos_raw[:, :, 0:HALF])
        nc.gpsimd.tensor_copy(out=table_1[:, :, HALF:DR], in_=sin_raw[:, :, HALF:DR])
        nc.gpsimd.tensor_scalar(
            out=table_2[:, :, 0:HALF], in0=sin_raw[:, :, 0:HALF], scalar1=-1.0, scalar2=0.0,
            op0=ALU.mult, op1=ALU.add,
        )
        nc.gpsimd.tensor_copy(out=table_2[:, :, HALF:DR], in_=cos_raw[:, :, HALF:DR])

        x_codes = keep.tile([P, TILES, W], U32, name="x_codes", align_bytes=64)
        x_scales = keep.tile([P, TILES, W], U8, name="x_scales", align_bytes=64)
        wkv_codes = keep.tile([P, 4, W], U32, name="wkv_codes", align_bytes=64)
        wkv_scales = keep.tile([P, 4, W], U8, name="wkv_scales", align_bytes=64)
        cq_codes = keep.tile([P, TILES, 3 * P], U32, name="cq_codes", align_bytes=64)
        cq_scales = keep.tile([P, TILES, 3 * P], U8, name="cq_scales", align_bytes=64)
        gain_q = const.tile([P, QR], BF16, name="gain_q")
        gain_kv = const.tile([P, W], BF16, name="gain_kv")

        units = []
        for g in range(4):
            units.append((wkv_raw[g][:], wkv_codes[:, g, :], wkv_scales[:, g, :], None))
        wa_codes, wa_scales = [], []
        for g in range(4):
            chunk = raw_pool.tile([P, 4, QR], BF16, tag="raw", name="wa_raw%d" % g)
            if g == 0:
                for c in range(3):
                    for u in range(2):
                        nc.sync.dma_start(
                            out=chunk[:, 2 * u:2 * u + 2, W * c:W * c + W],
                            in_=wq_a[256 * u:256 * u + 256, W * c:W * c + W].rearrange("(q e) c -> q e c", e=2),
                        )
            else:
                nc.sync.dma_start(
                    out=chunk[:].rearrange("p (u e) c -> p u e c", u=2),
                    in_=wq_a[512 * g:512 * g + 512, :].rearrange("(u q e) c -> q u e c", u=2, e=2),
                )
            wa_codes.append(code_pool.tile([P, QR], U32, tag="codes", name="wa_codes%d" % g, align_bytes=64))
            wa_scales.append(code_pool.tile([P, QR], U8, tag="scales", name="wa_scales%d" % g, align_bytes=64))
            for c in range(3):
                cols = slice(W * c, W * c + W)
                units.append((chunk[:, :, cols], wa_codes[g][:, cols], wa_scales[g][:, cols], ("a", g, c)))
        wb_codes, wb_scales = {}, {}
        for half in range(2):
            chunks = []
            for g in range(3):
                chunk = raw_pool.tile([P, 4, QR], BF16, tag="raw", name="wb_raw%d%d" % (half, g))
                nc.sync.dma_start(
                    out=chunk[:],
                    in_=wq_b[512 * g:512 * g + 512, QR * half:QR * half + QR].rearrange("(j p) n -> p j n", p=P),
                )
                chunks.append(chunk)
                wb_codes[(half, g)] = code_pool.tile(
                    [P, QR], U32, tag="codes", name="wb_codes%d%d" % (half, g), align_bytes=64
                )
                wb_scales[(half, g)] = code_pool.tile(
                    [P, QR], U8, tag="scales", name="wb_scales%d%d" % (half, g), align_bytes=64
                )
            for c in range(3):
                cols = slice(W * c, W * c + W)
                for g in range(3):
                    units.append((
                        chunks[g][:, :, cols], wb_codes[(half, g)][:, cols], wb_scales[(half, g)][:, cols],
                        ("q", 3 * half + c, g),
                    ))

        a_bank = {}
        q_bank = {}
        grouped = {}
        done = {"copied": 0, "quantised": 0, "multiplied": 0}

        def stage1_pass(t, c, g):
            cols = slice(W * c, W * c + W)
            nc.tensor.matmul_mx(
                out=a_bank[(t, c)][:],
                lhsT=x_codes[:, t, P * g:P * g + P].bitcast(FP8X4),
                lhsT_scale=x_scales[:, t, P * g:P * g + P],
                rhs=wa_codes[g][:, cols].bitcast(FP8X4),
                rhs_scale=wa_scales[g][:, cols],
                start=(g == 0),
                stop=(g == 3),
            )

        def regroup_next():
            k = done["copied"]
            if k >= len(units):
                return
            done["copied"] = k + 1
            grouped[k] = grouped_pool.tile([P, 4 * W], BF16, tag="grouped", name="grouped%d" % k, align_bytes=64)
            dst = grouped[k][:].rearrange("p (c i t) -> p c t i", i=4, t=4)
            src = units[k][0].rearrange("p t (c i) -> p c t i", i=4)
            if COPY_ENGINE[k] == "S":
                nc.scalar.copy(out=dst, in_=src)
            else:
                nc.vector.tensor_copy(out=dst, in_=src)

        def quantise_next():
            k = done["quantised"]
            if k >= len(units):
                return
            done["quantised"] = k + 1
            nc.vector.quantize_mx(out=units[k][1].bitcast(FP8X4), scales=units[k][2], in_=grouped[k][:])

        def multiply_next():
            k = done["multiplied"]
            if k >= len(units):
                return
            done["multiplied"] = k + 1
            what = units[k][3]
            if what is None:
                return
            if what[0] == "a":
                g, c = what[1], what[2]
                for t in range(TILES):
                    if (t, c) in EARLY_BANKS:
                        if g == 0:
                            a_bank[(t, c)] = psum.tile([P, W], F32, tag="bank", name="a%d%d" % (t, c))
                        stage1_pass(t, c, g)
            else:
                s, g = what[1], what[2]
                half, c = divmod(s, 3)
                cols = slice(W * c, W * c + W)
                for t in range(TILES):
                    if g == 0:
                        q_bank[(s, t)] = psum.tile([P, W], F32, tag="bank", name="q%d%d" % (s, t))
                    nc.tensor.matmul_mx(
                        out=q_bank[(s, t)][:],
                        lhsT=cq_codes[:, t, P * g:P * g + P].bitcast(FP8X4),
                        lhsT_scale=cq_scales[:, t, P * g:P * g + P],
                        rhs=wb_codes[(half, g)][:, cols].bitcast(FP8X4),
                        rhs_scale=wb_scales[(half, g)][:, cols],
                        start=(g == 0),
                        stop=(g == 2),
                    )

        def advance():
            regroup_next()
            quantise_next()
            multiply_next()

        x_grouped = {}
        x_bank = {}

        def x_transpose(t):
            words = x_raw[t][:].bitcast(F32)
            x_grouped[t] = grouped_pool.tile([P, 4 * W], BF16, tag="grouped", name="x_grouped%d" % t, align_bytes=64)
            for pair in range(2):
                x_bank[(t, pair)] = psum.tile([P, 4, P], F32, tag="bank", name="x_bank%d%d" % (t, pair))
                for i in range(4):
                    w0 = W * pair + P * i
                    nc.tensor.transpose(out=x_bank[(t, pair)][:, i, :], in_=words[:, w0:w0 + P], identity=ident_f32[:])
            for pair in range(2):
                dst = x_grouped[t][:].bitcast(F32)[:, W * pair:W * pair + W].rearrange("p (g r u) -> p g r u", g=2, u=2)
                nc.scalar.copy(out=dst, in_=x_bank[(t, pair)][:].rearrange("p (g u) r -> p g r u", u=2))

        def x_quantise(t):
            nc.vector.quantize_mx(out=x_codes[:, t, :].bitcast(FP8X4), scales=x_scales[:, t, :], in_=x_grouped[t][:])

        def spread_gains(c):
            bank = psum.tile([P, W], F32, tag="bank", name="gain_bank%d" % c)
            nc.tensor.matmul(out=bank[:], lhsT=ones[:], rhs=gain_rows[:, W * c:W * c + W], start=True, stop=True)
            if c < 3:
                nc.scalar.copy(out=gain_q[:, W * c:W * c + W], in_=bank[:])
            else:
                nc.scalar.copy(out=gain_kv[:], in_=bank[:])

        cq = {}
        sums = {}
        rms = {}
        cq_bank = {}
        cq_grouped = {}
        cq_codes_flat = cq_codes[:].rearrange("p t w -> p (t w)")
        cq_scales_flat = cq_scales[:].rearrange("p t w -> p (t w)")

        def squares(t, thirds):
            if t not in sums:
                sums[t] = stat.tile([P, 4], F32, tag="sums", name="sums%d" % t)
            for c in thirds:
                junk = junk_pool.tile([P, W], BF16, tag="junk", name="junk")
                nc.scalar.activation(
                    out=junk[:], in_=a_bank[(t, c)][:], func=ACT.Square, accum_out=sums[t][:, c:c + 1]
                )

        def root_mean_square(t):
            total = stat.tile([P, 1], F32, tag="total", name="total%d" % t)
            copy3 = stat.tile([P, 4], F32, tag="copy3", name="copy3")
            nc.scalar.activation(out=copy3[:, 0:3], in_=sums[t][:, 0:3], func=ACT.Copy, accum_out=total[:])
            rms[t] = stat.tile([P, 1], F32, tag="rms", name="rms%d" % t)
            nc.scalar.activation(out=rms[t][:], in_=total[:], func=ACT.Sqrt, bias=eps[:, 0:1], scale=1.0 / QR)

        def scale_cq(t):
            rstd = stat.tile([P, 1], F32, tag="rstd", name="rstd%d" % t)
            nc.vector.reciprocal(out=rstd[:], in_=rms[t][:])
            cq[t] = cq_pool.tile([P, QR], BF16, tag="cq", name="cq%d" % t)
            for c in range(3):
                cols = slice(W * c, W * c + W)
                nc.vector.scalar_tensor_tensor(
                    out=cq[t][:, cols], in0=a_bank[(t, c)][:], scalar=rstd[:, 0:1], in1=gain_q[:, cols],
                    op0=ALU.mult, op1=ALU.mult,
                )

        def late_bank(t, c):
            a_bank[(t, c)] = psum.tile([P, W], F32, tag="bank", name="a%d%d" % (t, c))
            for g in range(4):
                stage1_pass(t, c, g)

        def cq_transpose(pair):
            cq_bank[pair] = psum.tile([P, 8, P], BF16, tag="bank", name="cq_bank%d" % pair)
            for h in range(2):
                t, g = divmod(2 * pair + h, 3)
                for j in range(4):
                    k0 = 512 * g + P * j
                    nc.tensor.transpose(
                        out=cq_bank[pair][:, 4 * h + j, :], in_=cq[t][:, k0:k0 + P], identity=ident_bf16[:]
                    )

        def cq_copy(pair):
            cq_grouped[pair] = cqg_pool.tile([P, 2 * W], BF16, tag="cqg", name="cq_grouped%d" % pair, align_bytes=64)
            dst = cq_grouped[pair][:].rearrange("p (h r j) -> p h r j", h=2, j=4)
            src = cq_bank[pair][:].rearrange("p (h j) r -> p h r j", h=2)
            if CQ_COPY_ENGINE[pair] == "S":
                nc.scalar.copy(out=dst, in_=src)
            else:
                nc.vector.tensor_copy(out=dst, in_=src)

        def cq_quantise(pair):
            nc.vector.quantize_mx(
                out=cq_codes_flat[:, 2 * P * pair:2 * P * pair + 2 * P].bitcast(FP8X4),
                scales=cq_scales_flat[:, 2 * P * pair:2 * P * pair + 2 * P],
                in_=cq_grouped[pair][:],
            )

        products = {}
        out_tile = {}

        def rope_products(key, bank, first_slot, t):
            n = len(range(first_slot, 8, 3))
            halves = bank[:].rearrange("p (s w) -> p s w", w=HALF)
            shape = [P, n, 2, HALF]
            x1 = halves[:, 2 * first_slot:16:6, :].unsqueeze(2).to_broadcast(shape)
            x2 = halves[:, 2 * first_slot + 1:16:6, :].unsqueeze(2).to_broadcast(shape)
            t1 = table_1[:, t, :].rearrange("p (h w) -> p h w", h=2).unsqueeze(1).to_broadcast(shape)
            t2 = table_2[:, t, :].rearrange("p (h w) -> p h w", h=2).unsqueeze(1).to_broadcast(shape)
            p1 = rope_pool.tile([P, 3, 2, HALF], F32, tag="p1", name="p1")
            p2 = rope_pool.tile([P, 3, 2, HALF], F32, tag="p2", name="p2")
            nc.vector.tensor_tensor(out=p1[:, 0:n], in0=x1, in1=t1, op=ALU.mult)
            nc.vector.tensor_tensor(out=p2[:, 0:n], in0=x2, in1=t2, op=ALU.mult)
            products[key] = (p1, p2, n, first_slot)

        def rope_sum(key):
            p1, p2, n, first_slot = products[key]
            slots = out_tile[key][:].rearrange("p (s h w) -> p s h w", h=2, w=HALF)
            nc.vector.tensor_tensor(out=slots[:, first_slot:8:3], in0=p1[:, 0:n], in1=p2[:, 0:n], op=ALU.add)

        kv_bank = {}
        kv_rms = {}

        def kv_passes(t):
            kv_bank[t] = psum.tile([P, W], F32, tag="bank", name="kv%d" % t)
            for g in range(4):
                nc.tensor.matmul_mx(
                    out=kv_bank[t][:],
                    lhsT=x_codes[:, t, P * g:P * g + P].bitcast(FP8X4),
                    lhsT_scale=x_scales[:, t, P * g:P * g + P],
                    rhs=wkv_codes[:, g, :].bitcast(FP8X4),
                    rhs_scale=wkv_scales[:, g, :],
                    start=(g == 0),
                    stop=(g == 3),
                )

        def kv_root_mean_square(t):
            total = stat.tile([P, 1], F32, tag="total", name="kv_total%d" % t)
            junk = junk_pool.tile([P, W], BF16, tag="junk", name="junk")
            nc.scalar.activation(out=junk[:, 0:KVR], in_=kv_bank[t][:, 0:KVR], func=ACT.Square, accum_out=total[:])
            kv_rms[t] = stat.tile([P, 1], F32, tag="rms", name="kv_rms%d" % t)
            nc.scalar.activation(out=kv_rms[t][:], in_=total[:], func=ACT.Sqrt, bias=eps[:, 0:1], scale=1.0 / KVR)

        def kv_finish(t):
            rstd = stat.tile([P, 1], F32, tag="rstd", name="kv_rstd%d" % t)
            nc.vector.reciprocal(out=rstd[:], in_=kv_rms[t][:])
            out_tile[("kv", t)] = out_pool.tile([P, W], F32, tag="out", name="kv_out%d" % t)
            nc.vector.scalar_tensor_tensor(
                out=out_tile[("kv", t)][:, 0:KVR], in0=kv_bank[t][:, 0:KVR], scalar=rstd[:, 0:1],
                in1=gain_kv[:, 0:KVR], op0=ALU.mult, op1=ALU.mult,
            )
            rope_products(("kv", t), kv_bank[t], KV_ROPE_SLOT, t)
            rope_sum(("kv", t))
            nc.sync.dma_start(out=out_view[:, t, NQ:NQ + KV], in_=out_tile[("kv", t)][:])

        def plain_columns_out(s, t):
            rope_class = FIRST_ROPE_SLOT[s % 3] % 3
            out_tile[(s, t)] = out_pool.tile([P, W], F32, tag="out", name="q_out%d%d" % (s, t))
            src = q_bank[(s, t)][:].rearrange("p (s w) -> p s w", w=DR)
            dst = out_tile[(s, t)][:].rearrange("p (s w) -> p s w", w=DR)
            for r in range(3):
                if r != rope_class:
                    nc.scalar.copy(out=dst[:, r:8:3, :], in_=src[:, r:8:3, :])

        def q_store(s, t):
            rope_sum((s, t))
            nc.sync.dma_start(out=out_view[:, t, W * s:W * s + W], in_=out_tile[(s, t)][:])

        x_transpose(0)
        x_transpose(1)
        x_quantise(0)
        regroup_next()
        x_transpose(2)
        x_quantise(1)
        regroup_next()
        quantise_next()
        multiply_next()
        x_transpose(3)
        x_quantise(2)
        advance()
        x_quantise(3)
        for c in (3, 0, 1, 2):
            spread_gains(c)
        advance()
        advance()
        for t in range(TILES):
            kv_passes(t)
        advance()
        kv_root_mean_square(0)
        kv_root_mean_square(1)
        advance()
        kv_root_mean_square(2)
        kv_finish(0)
        advance()
        kv_root_mean_square(3)
        kv_finish(1)
        advance()
        kv_finish(2)
        advance()
        kv_finish(3)

        regroup_next()
        for k in range(7):
            advance()

        squares(0, (0, 1, 2))
        root_mean_square(0)
        quantise_next()
        squares(1, (0, 1, 2))
        root_mean_square(1)
        scale_cq(0)
        late_bank(2, 2)
        late_bank(3, 0)
        late_bank(3, 1)
        squares(2, (0, 1))
        scale_cq(1)
        late_bank(3, 2)
        squares(2, (2,))
        root_mean_square(2)
        cq_transpose(0)
        squares(3, (0,))
        scale_cq(2)
        squares(3, (1, 2))
        root_mean_square(3)
        cq_transpose(1)
        cq_transpose(2)
        cq_copy(0)
        scale_cq(3)
        cq_transpose(3)
        cq_copy(1)
        cq_quantise(0)
        cq_transpose(4)
        cq_transpose(5)
        cq_copy(2)
        cq_copy(4)
        cq_quantise(1)
        cq_copy(3)
        cq_copy(5)
        cq_quantise(2)
        cq_quantise(4)
        cq_quantise(3)
        cq_quantise(5)
        multiply_next()
        advance()
        advance()

        banks = [(s, t) for s in range(6) for t in range(TILES)]
        for n in range(len(banks) + 2):
            if n < len(banks):
                plain_columns_out(*banks[n])
            if 1 <= n <= len(banks):
                s, t = banks[n - 1]
                rope_products((s, t), q_bank[(s, t)], FIRST_ROPE_SLOT[s % 3], t)
            if n >= 2:
                q_store(*banks[n - 2])
            if n % 4 != 3:
                advance()
